import numpy as np
import ml_dtypes


def mxq(x, axis, fmt="e4m3"):
    dtype, down = {"e4m3": (ml_dtypes.float8_e4m3fn, 7), "e5m2": (ml_dtypes.float8_e5m2, 14)}[fmt]
    v = np.moveaxis(np.asarray(x, np.float32).astype(ml_dtypes.bfloat16).astype(np.float64), axis, -1)
    blocks = v.reshape(v.shape[:-1] + (-1, 32))
    amax = np.abs(blocks).max(-1, keepdims=True)
    byte = np.maximum(np.where(amax > 0, np.frexp(amax)[1] - 1 + 127, 0) - down, 1)
    scale = np.exp2(byte - 127.0)
    codes = (blocks / scale).astype(np.float32).astype(dtype).astype(np.float64)
    return np.moveaxis((codes * scale).reshape(v.shape), -1, axis)


WIDE = False


def mx_kscale(k):
    if not WIDE:
        return np.ones(k)
    levels = np.array([10, -10, 5, -5, 0])
    a = np.random.permutation(np.resize(levels, k // 512 * 4)).reshape(k // 512, 4)
    idx = np.arange(k)
    return np.exp2(a[idx // 512, idx % 128 // 32])


BF16 = ml_dtypes.bfloat16


def bf(x):
    return np.asarray(x, np.float32).astype(BF16)


def f64(x):
    return np.asarray(x).astype(np.float64)


B, D_IN, HID, OUT = 512, 1024, 4096, 1024


def setup_inputs():
    s, t = mx_kscale(D_IN), mx_kscale(HID)
    u = np.concatenate([s, t])
    return {"x": bf(np.random.standard_normal((B, D_IN)) * s),
            "W1": bf(np.random.standard_normal((HID, D_IN)) / np.sqrt(D_IN) / s[None, :] * t[:, None]),
            "b1": bf(np.random.standard_normal(HID) * 0.3 * t),
            "W2": bf(np.random.standard_normal((OUT, D_IN + HID)) / np.sqrt(D_IN + HID) / u[None, :]),
            "b2": bf(np.random.standard_normal(OUT) * 0.3)}


def reference(x, W1, b1, W2, b2):
    xq = mxq(f64(x), 1, "e4m3")
    h1 = np.maximum((xq @ mxq(f64(W1), 1, "e4m3").T) + f64(b1), 0.0)
    concat = np.concatenate([xq, mxq(h1, 1, "e4m3")], axis=1)
    return (concat @ mxq(f64(W2), 1, "e4m3").T) + f64(b2)

@@ -1,0 +1,271 @@
+from contextlib import ExitStack
+
+import concourse.mybir as mybir
+from concourse.masks import make_identity
+
+F32 = mybir.dt.float32
+BF16 = mybir.dt.bfloat16
+U32 = mybir.dt.uint32
+U8 = mybir.dt.uint8
+FP8X4 = mybir.dt.float8_e4m3fn_x4
+ACT = mybir.ActivationFunctionType
+ALU = mybir.AluOpType
+
+P = 128
+B, D_IN, HID, OUT = 512, 1024, 4096, 1024
+FLOPS = 2 * B * (D_IN * HID + (D_IN + HID) * OUT)
+
+MANUAL = True
+RAW_BUFS = 9
+N_UNITS = 19
+
+
+def tile_dpn_kernel(tc, x, W1, b1, W2, b2, out):
+    nc = tc.nc
+    with ExitStack() as ctx:
+        const = ctx.enter_context(tc.tile_pool(name="const", bufs=1))
+        keep = ctx.enter_context(tc.tile_pool(name="keep", bufs=1))
+        rawp = ctx.enter_context(tc.tile_pool(name="rawp", bufs=RAW_BUFS))
+        grpp = ctx.enter_context(tc.tile_pool(name="grpp", bufs=3))
+        w1p = ctx.enter_context(tc.tile_pool(name="w1p", bufs=3))
+        hpp = ctx.enter_context(tc.tile_pool(name="hpp", bufs=3))
+        ostp = ctx.enter_context(tc.tile_pool(name="ostp", bufs=4))
+        psum = ctx.enter_context(tc.psum_pool(name="psum", bufs=4))
+        if MANUAL:
+            ctx.enter_context(tc.manual_schedule())
+
+        xc = keep.tile([P, 1024], U32, name="xc", align_bytes=64)
+        xs = keep.tile([P, 1024], U8, name="xs", align_bytes=64)
+        hc = keep.tile([P, 4096], U32, name="hc", align_bytes=64)
+        hs = keep.tile([P, 4096], U8, name="hs", align_bytes=64)
+        w2c = keep.tile([P, 10240], U32, name="w2c", align_bytes=64)
+        w2s = keep.tile([P, 10240], U8, name="w2s", align_bytes=64)
+
+        raws = {}
+        banks = {}
+        grps = {}
+        codes = {0: (xc[:], xs[:])}
+        for q in range(10):
+            codes[9 + q] = (
+                w2c[:, q * 1024 : (q + 1) * 1024],
+                w2s[:, q * 1024 : (q + 1) * 1024],
+            )
+
+        def load(k):
+            raw = rawp.tile([P, 4096], BF16, name="raw", tag="raw")
+            raws[k] = raw
+            if k == 0:
+                src = x.rearrange("(s p) k -> p s k", p=P)
+                dst = raw[:].rearrange("p (s k) -> p s k", s=4)
+                nc.sync.dma_start(out=dst[:, 0:2, :], in_=src[:, 0:2, :])
+                nc.sync.dma_start(out=dst[:, 2:4, :], in_=src[:, 2:4, :])
+            elif k < 9:
+                j = k - 1
+                src = W1[512 * j : 512 * (j + 1), :].rearrange(
+                    "(u p e) k -> p u (e k)", u=2, e=2
+                )
+                dst = raw[:].rearrange("p (u f) -> p u f", u=2)
+                if k == 1:
+                    nc.sync.dma_start(out=dst[:, 0:1, :], in_=src[:, 0:1, :])
+                    nc.sync.dma_start(out=dst[:, 1:2, :], in_=src[:, 1:2, :])
+                else:
+                    nc.sync.dma_start(out=dst, in_=src)
+            else:
+                n, c = divmod(k - 9, 5)
+                src = W2[
+                    512 * n : 512 * (n + 1), 1024 * c : 1024 * (c + 1)
+                ].rearrange("(s p) k -> p s k", p=P)
+                dst = raw[:].rearrange("p (s k) -> p s k", s=4)
+                nc.sync.dma_start(out=dst, in_=src)
+
+        def transposes(k):
+            rw = raws[k][:].bitcast(F32)
+            bl = []
+            for s in range(4):
+                bank = psum.tile([P, 512], F32, name="tb", tag="tb")
+                for q in range(4):
+                    nc.tensor.transpose(
+                        bank[:, q * P : (q + 1) * P],
+                        rw[:, s * 512 + q * P : s * 512 + (q + 1) * P],
+                        ident[:],
+                    )
+                bl.append(bank)
+            banks[k] = bl
+            grps[k] = grpp.tile([P, 4096], BF16, name="grp", tag="grp", align_bytes=64)
+
+        def evac(k, s, eng):
+            dst = grps[k][:].bitcast(F32).rearrange(
+                "p (g s r u) -> p g s r u", g=2, s=4, u=2
+            )[:, :, s]
+            src = banks[k][s][:].rearrange("p (g u r) -> p g r u", g=2, u=2)
+            if eng == "V":
+                nc.vector.tensor_copy(out=dst, in_=src)
+            else:
+                nc.scalar.copy(out=dst, in_=src)
+
+        def quant(k):
+            if 1 <= k < 9:
+                w1c = w1p.tile([P, 1024], U32, name="w1c", tag="w1c", align_bytes=64)
+                w1s = w1p.tile([P, 1024], U8, name="w1s", tag="w1s", align_bytes=64)
+                codes[k] = (w1c[:], w1s[:])
+            cd, sc = codes[k]
+            nc.vector.quantize_mx(out=cd.bitcast(FP8X4), scales=sc, in_=grps[k][:])
+
+        accs = {}
+        hps = {}
+        hgs = {}
+
+        def mm1(j):
+            cd, sc = codes[1 + j]
+            al = []
+            for t in range(4):
+                acc = psum.tile([P, 512], F32, name="mb", tag="mb")
+                for g in range(2):
+                    cols = slice(g * 512 + t * P, g * 512 + (t + 1) * P)
+                    nc.tensor.matmul_mx(
+                        out=acc[:],
+                        lhsT=cd[:, cols].bitcast(FP8X4),
+                        lhsT_scale=sc[:, cols],
+                        rhs=xc[:, g * 512 : (g + 1) * 512].bitcast(FP8X4),
+                        rhs_scale=xs[:, g * 512 : (g + 1) * 512],
+                        start=(g == 0),
+                        stop=(g == 1),
+                    )
+                al.append(acc)
+            accs[j] = al
+            hps[j] = hpp.tile([P, 2048], BF16, name="hp", tag="hp")
+
+        def relu(j, t, eng):
+            dst = hps[j][:, t * 512 : (t + 1) * 512]
+            bias = b1col[:, 4 * j + t : 4 * j + t + 1]
+            if eng == "V":
+                nc.vector.tensor_scalar(
+                    out=dst, in0=accs[j][t][:], scalar1=bias, scalar2=0.0,
+                    op0=ALU.add, op1=ALU.max,
+                )
+            else:
+                nc.scalar.activation(
+                    out=dst, in_=accs[j][t][:], func=ACT.Relu, bias=bias, scale=1.0
+                )
+
+        def regroup(j):
+            hg = hpp.tile([P, 2048], BF16, name="hg", tag="hg", align_bytes=64)
+            hgs[j] = hg
+            nc.vector.tensor_copy(
+                out=hg[:].rearrange("p (c i t) -> p c t i", i=4, t=4),
+                in_=hps[j][:].rearrange("p (t c i) -> p c t i", t=4, i=4),
+            )
+
+        def quant_h(j):
+            nc.vector.quantize_mx(
+                out=hc[:, j * 512 : (j + 1) * 512].bitcast(FP8X4),
+                scales=hs[:, j * 512 : (j + 1) * 512],
+                in_=hgs[j][:],
+            )
+
+        acc2 = {}
+
+        def mm2(n, c):
+            if c == 0:
+                acc2[n] = [
+                    psum.tile([P, 512], F32, name="mb", tag="mb") for bt in range(4)
+                ]
+            for bt in range(4):
+                for gg in (2 * c, 2 * c + 1):
+                    if gg < 2:
+                        lc, ls, base = xc, xs, gg * 512
+                    else:
+                        lc, ls, base = hc, hs, (gg - 2) * 512
+                    cols = slice(base + bt * P, base + (bt + 1) * P)
+                    rcols = slice(n * 5120 + gg * 512, n * 5120 + (gg + 1) * 512)
+                    nc.tensor.matmul_mx(
+                        out=acc2[n][bt][:],
+                        lhsT=lc[:, cols].bitcast(FP8X4),
+                        lhsT_scale=ls[:, cols],
+                        rhs=w2c[:, rcols].bitcast(FP8X4),
+                        rhs_scale=w2s[:, rcols],
+                        start=(gg == 0),
+                        stop=(gg == 9),
+                    )
+
+        def finish(n, bt):
+            ost = ostp.tile([P, 512], F32, name="ost", tag="ost")
+            nc.vector.tensor_tensor(
+                out=ost[:], in0=acc2[n][bt][:], in1=b2bc[:, n * 512 : (n + 1) * 512],
+                op=ALU.add,
+            )
+            nc.sync.dma_start(
+                out=out[bt * P : (bt + 1) * P, n * 512 : (n + 1) * 512], in_=ost[:]
+            )
+
+        b1z = const.tile([P, 256], BF16, name="b1z")
+        b2z = const.tile([P, OUT], BF16, name="b2z")
+        ones = const.tile([P, P], BF16, name="ones")
+        ident = const.tile([P, P], F32, name="ident")
+        b1col = const.tile([P, 32], F32, name="b1col")
+        b2bc = const.tile([P, OUT], F32, name="b2bc")
+        nc.vector.memset(b1z[:], 0.0)
+        nc.vector.memset(b2z[:], 0.0)
+        nc.vector.memset(ones[:], 1.0)
+        nc.scalar.dma_start(out=b1z[0:16, :], in_=b1.rearrange("(a w) -> a w", a=16))
+        nc.scalar.dma_start(out=b2z[0:1, :], in_=b2.rearrange("(o n) -> o n", o=1))
+        make_identity(nc, ident[:])
+
+        for k in range(RAW_BUFS):
+            load(k)
+
+        def next_load(k):
+            if k + RAW_BUFS < N_UNITS:
+                load(k + RAW_BUFS)
+
+        transposes(0)
+        next_load(0)
+        evac(0, 0, "V")
+        evac(0, 1, "S")
+        evac(0, 2, "V")
+        evac(0, 3, "S")
+        b1ps = psum.tile([P, 512], F32, name="mb", tag="mb")
+        nc.tensor.transpose(b1ps[:, 0:P], b1z[:].bitcast(F32), ident[:])
+        nc.vector.tensor_copy(out=b1col[:], in_=b1ps[:, 0:16].bitcast(BF16))
+        for n in range(2):
+            b2ps = psum.tile([P, 512], F32, name="mb", tag="mb")
+            nc.tensor.matmul(
+                out=b2ps[:], lhsT=ones[:], rhs=b2z[:, n * 512 : (n + 1) * 512],
+                start=True, stop=True,
+            )
+            nc.scalar.copy(out=b2bc[:, n * 512 : (n + 1) * 512], in_=b2ps[:])
+        quant(0)
+        transposes(1)
+        next_load(1)
+        evac(1, 0, "V")
+        evac(1, 1, "S")
+        evac(1, 2, "V")
+        evac(1, 3, "S")
+        quant(1)
+
+        for p in range(18):
+            k = p + 2
+            if k < N_UNITS:
+                transposes(k)
+                next_load(k)
+            if p < 8:
+                mm1(p)
+            else:
+                mm2(*divmod(p - 8, 5))
+            if k < N_UNITS:
+                evac(k, 0, "V")
+                evac(k, 1, "S")
+                evac(k, 2, "S")
+                evac(k, 3, "S")
+            if 1 <= p <= 8:
+                regroup(p - 1)
+            if 2 <= p <= 9:
+                quant_h(p - 2)
+            if k < N_UNITS:
+                quant(k)
+            if p < 8:
+                for t in range(4):
+                    relu(p, t, "V" if (t == 3 and p % 2 == 1) else "S")
+            if p == 12 or p == 17:
+                for bt in range(4):
+                    finish((p - 8) // 5, bt)

@@ -15,8 +15,7 @@ P = 128
 B, D_IN, HID, OUT = 512, 1024, 4096, 1024
 FLOPS = 2 * B * (D_IN * HID + (D_IN + HID) * OUT)
 
-MANUAL = True
-RAW_BUFS = 9
+RAW_BUFS = 8
 N_UNITS = 19
 
 
@@ -27,12 +26,11 @@ def tile_dpn_kernel(tc, x, W1, b1, W2, b2, out):
         keep = ctx.enter_context(tc.tile_pool(name="keep", bufs=1))
         rawp = ctx.enter_context(tc.tile_pool(name="rawp", bufs=RAW_BUFS))
         grpp = ctx.enter_context(tc.tile_pool(name="grpp", bufs=3))
-        w1p = ctx.enter_context(tc.tile_pool(name="w1p", bufs=3))
+        w1p = ctx.enter_context(tc.tile_pool(name="w1p", bufs=4))
         hpp = ctx.enter_context(tc.tile_pool(name="hpp", bufs=3))
         ostp = ctx.enter_context(tc.tile_pool(name="ostp", bufs=4))
         psum = ctx.enter_context(tc.psum_pool(name="psum", bufs=4))
-        if MANUAL:
-            ctx.enter_context(tc.manual_schedule())
+        ctx.enter_context(tc.manual_schedule())
 
         xc = keep.tile([P, 1024], U32, name="xc", align_bytes=64)
         xs = keep.tile([P, 1024], U8, name="xs", align_bytes=64)
@@ -51,89 +49,108 @@ def tile_dpn_kernel(tc, x, W1, b1, W2, b2, out):
                 w2s[:, q * 1024 : (q + 1) * 1024],
             )
 
+        def is_w1(k):
+            return 1 <= k < 9
+
         def load(k):
             raw = rawp.tile([P, 4096], BF16, name="raw", tag="raw")
             raws[k] = raw
+            dst = raw[:].rearrange("p (s k) -> p s k", s=4)
             if k == 0:
                 src = x.rearrange("(s p) k -> p s k", p=P)
-                dst = raw[:].rearrange("p (s k) -> p s k", s=4)
-                nc.sync.dma_start(out=dst[:, 0:2, :], in_=src[:, 0:2, :])
-                nc.sync.dma_start(out=dst[:, 2:4, :], in_=src[:, 2:4, :])
+                for s in range(4):
+                    nc.sync.dma_start(out=dst[:, s, :], in_=src[:, s, :])
+            elif k == 1:
+                src = W1[0:512, :].rearrange("(u p e) k -> p u e k", u=2, e=2)
+                for s in range(4):
+                    nc.sync.dma_start(out=dst[:, s, :], in_=src[:, s // 2, s % 2, :])
             elif k < 9:
                 j = k - 1
                 src = W1[512 * j : 512 * (j + 1), :].rearrange(
                     "(u p e) k -> p u (e k)", u=2, e=2
                 )
-                dst = raw[:].rearrange("p (u f) -> p u f", u=2)
-                if k == 1:
-                    nc.sync.dma_start(out=dst[:, 0:1, :], in_=src[:, 0:1, :])
-                    nc.sync.dma_start(out=dst[:, 1:2, :], in_=src[:, 1:2, :])
-                else:
-                    nc.sync.dma_start(out=dst, in_=src)
+                nc.sync.dma_start(
+                    out=raw[:].rearrange("p (u f) -> p u f", u=2), in_=src
+                )
             else:
                 n, c = divmod(k - 9, 5)
                 src = W2[
                     512 * n : 512 * (n + 1), 1024 * c : 1024 * (c + 1)
                 ].rearrange("(s p) k -> p s k", p=P)
-                dst = raw[:].rearrange("p (s k) -> p s k", s=4)
                 nc.sync.dma_start(out=dst, in_=src)
 
-        def transposes(k):
-            rw = raws[k][:].bitcast(F32)
-            bl = []
-            for s in range(4):
-                bank = psum.tile([P, 512], F32, name="tb", tag="tb")
-                for q in range(4):
-                    nc.tensor.transpose(
-                        bank[:, q * P : (q + 1) * P],
-                        rw[:, s * 512 + q * P : s * 512 + (q + 1) * P],
-                        ident[:],
-                    )
-                bl.append(bank)
-            banks[k] = bl
+        def start_unit(k):
+            banks[k] = []
             grps[k] = grpp.tile([P, 4096], BF16, name="grp", tag="grp", align_bytes=64)
+            if is_w1(k):
+                w1c = w1p.tile([P, 1024], U32, name="w1c", tag="w1c", align_bytes=64)
+                w1s = w1p.tile([P, 1024], U8, name="w1s", tag="w1s", align_bytes=64)
+                codes[k] = (w1c[:], w1s[:])
+
+        def transposes(k, s):
+            rw = raws[k][:].bitcast(F32)
+            bank = psum.tile([P, 512], F32, name="tb", tag="tb")
+            for q in range(4):
+                nc.tensor.transpose(
+                    bank[:, q * P : (q + 1) * P],
+                    rw[:, s * 512 + q * P : s * 512 + (q + 1) * P],
+                    ident[:],
+                )
+            banks[k].append(bank)
 
         def evac(k, s, eng):
-            dst = grps[k][:].bitcast(F32).rearrange(
-                "p (g s r u) -> p g s r u", g=2, s=4, u=2
-            )[:, :, s]
+            gw = grps[k][:].bitcast(F32)
+            if is_w1(k):
+                dst = gw[:, s * 512 : (s + 1) * 512].rearrange(
+                    "p (g r u) -> p g r u", g=2, u=2
+                )
+            else:
+                dst = gw.rearrange("p (g s r u) -> p g s r u", g=2, s=4, u=2)[:, :, s]
             src = banks[k][s][:].rearrange("p (g u r) -> p g r u", g=2, u=2)
             if eng == "V":
                 nc.vector.tensor_copy(out=dst, in_=src)
             else:
                 nc.scalar.copy(out=dst, in_=src)
 
-        def quant(k):
-            if 1 <= k < 9:
-                w1c = w1p.tile([P, 1024], U32, name="w1c", tag="w1c", align_bytes=64)
-                w1s = w1p.tile([P, 1024], U8, name="w1s", tag="w1s", align_bytes=64)
-                codes[k] = (w1c[:], w1s[:])
+        def quant_cols(k, lo, hi):
             cd, sc = codes[k]
-            nc.vector.quantize_mx(out=cd.bitcast(FP8X4), scales=sc, in_=grps[k][:])
+            nc.vector.quantize_mx(
+                out=cd[:, lo:hi].bitcast(FP8X4),
+                scales=sc[:, lo:hi],
+                in_=grps[k][:, 4 * lo : 4 * hi],
+            )
+
+        def quant(k, s_lo, s_hi):
+            if is_w1(k):
+                quant_cols(k, s_lo * 256, s_hi * 256)
+            elif s_hi - s_lo == 4:
+                quant_cols(k, 0, 1024)
+            else:
+                for g in range(2):
+                    quant_cols(k, g * 512 + s_lo * P, g * 512 + s_hi * P)
 
         accs = {}
         hps = {}
         hgs = {}
 
-        def mm1(j):
+        def mm1(j, t):
             cd, sc = codes[1 + j]
-            al = []
-            for t in range(4):
-                acc = psum.tile([P, 512], F32, name="mb", tag="mb")
-                for g in range(2):
-                    cols = slice(g * 512 + t * P, g * 512 + (t + 1) * P)
-                    nc.tensor.matmul_mx(
-                        out=acc[:],
-                        lhsT=cd[:, cols].bitcast(FP8X4),
-                        lhsT_scale=sc[:, cols],
-                        rhs=xc[:, g * 512 : (g + 1) * 512].bitcast(FP8X4),
-                        rhs_scale=xs[:, g * 512 : (g + 1) * 512],
-                        start=(g == 0),
-                        stop=(g == 1),
-                    )
-                al.append(acc)
-            accs[j] = al
-            hps[j] = hpp.tile([P, 2048], BF16, name="hp", tag="hp")
+            if t == 0:
+                accs[j] = []
+                hps[j] = hpp.tile([P, 2048], BF16, name="hp", tag="hp", bufs=5)
+            acc = psum.tile([P, 512], F32, name="mb", tag="mb")
+            for g in range(2):
+                cols = slice(t * 256 + g * P, t * 256 + (g + 1) * P)
+                nc.tensor.matmul_mx(
+                    out=acc[:],
+                    lhsT=cd[:, cols].bitcast(FP8X4),
+                    lhsT_scale=sc[:, cols],
+                    rhs=xc[:, g * 512 : (g + 1) * 512].bitcast(FP8X4),
+                    rhs_scale=xs[:, g * 512 : (g + 1) * 512],
+                    start=(g == 0),
+                    stop=(g == 1),
+                )
+            accs[j].append(acc)
 
         def relu(j, t, eng):
             dst = hps[j][:, t * 512 : (t + 1) * 512]
@@ -165,28 +182,27 @@ def tile_dpn_kernel(tc, x, W1, b1, W2, b2, out):
 
         acc2 = {}
 
-        def mm2(n, c):
+        def mm2(n, c, bt):
             if c == 0:
-                acc2[n] = [
-                    psum.tile([P, 512], F32, name="mb", tag="mb") for bt in range(4)
-                ]
-            for bt in range(4):
-                for gg in (2 * c, 2 * c + 1):
-                    if gg < 2:
-                        lc, ls, base = xc, xs, gg * 512
-                    else:
-                        lc, ls, base = hc, hs, (gg - 2) * 512
-                    cols = slice(base + bt * P, base + (bt + 1) * P)
-                    rcols = slice(n * 5120 + gg * 512, n * 5120 + (gg + 1) * 512)
-                    nc.tensor.matmul_mx(
-                        out=acc2[n][bt][:],
-                        lhsT=lc[:, cols].bitcast(FP8X4),
-                        lhsT_scale=ls[:, cols],
-                        rhs=w2c[:, rcols].bitcast(FP8X4),
-                        rhs_scale=w2s[:, rcols],
-                        start=(gg == 0),
-                        stop=(gg == 9),
-                    )
+                if bt == 0:
+                    acc2[n] = []
+                acc2[n].append(psum.tile([P, 512], F32, name="mb", tag="mb"))
+            for gg in (2 * c, 2 * c + 1):
+                if gg < 2:
+                    lc, ls, base = xc, xs, gg * 512
+                else:
+                    lc, ls, base = hc, hs, (gg - 2) * 512
+                cols = slice(base + bt * P, base + (bt + 1) * P)
+                rcols = slice(n * 5120 + gg * 512, n * 5120 + (gg + 1) * 512)
+                nc.tensor.matmul_mx(
+                    out=acc2[n][bt][:],
+                    lhsT=lc[:, cols].bitcast(FP8X4),
+                    lhsT_scale=ls[:, cols],
+                    rhs=w2c[:, rcols].bitcast(FP8X4),
+                    rhs_scale=w2s[:, rcols],
+                    start=(gg == 0),
+                    stop=(gg == 9),
+                )
 
         def finish(n, bt):
             ost = ostp.tile([P, 512], F32, name="ost", tag="ost")
@@ -214,58 +230,93 @@ def tile_dpn_kernel(tc, x, W1, b1, W2, b2, out):
         for k in range(RAW_BUFS):
             load(k)
 
-        def next_load(k):
-            if k + RAW_BUFS < N_UNITS:
-                load(k + RAW_BUFS)
+        def evac_pattern(k):
+            if k < 2 or (k < 10 and k % 2 == 0):
+                return "VSVS"
+            return "SSVS"
 
-        transposes(0)
-        next_load(0)
-        evac(0, 0, "V")
-        evac(0, 1, "S")
-        evac(0, 2, "V")
-        evac(0, 3, "S")
+        def quant_parts(k):
+            if k < 2:
+                return 1
+            if k < 9:
+                return 2
+            return 4
+
+        def evac_quant(k, s):
+            evac(k, s, evac_pattern(k)[s])
+            step = quant_parts(k)
+            if (s + 1) % step == 0:
+                quant(k, s + 1 - step, s + 1)
+
+        def t_run(units):
+            prev = None
+            for k in units:
+                start_unit(k)
+                for s in range(4):
+                    if prev is not None:
+                        evac_quant(prev, s)
+                    transposes(k, s)
+                if k + RAW_BUFS < N_UNITS:
+                    load(k + RAW_BUFS)
+                prev = k
+            return prev
+
+        def drain(p, b):
+            if p < 8:
+                relu(p, b, "V" if (b == 3 and p % 2 == 0) else "S")
+            if p == 12 or p == 17:
+                finish((p - 8) // 5, b)
+            if b == 3:
+                if 2 <= p <= 7:
+                    quant_h(p - 2)
+                if 1 <= p <= 6:
+                    regroup(p - 1)
+                if p == 9:
+                    regroup(6)
+                    regroup(7)
+                    quant_h(6)
+                    quant_h(7)
+
+        def m_run(ps):
+            prev = None
+            for p in ps:
+                for b in range(4):
+                    if prev is not None:
+                        drain(prev, b)
+                    if p < 8:
+                        mm1(p, b)
+                    else:
+                        n, c = divmod(p - 8, 5)
+                        mm2(n, c, b)
+                prev = p
+            for b in range(4):
+                drain(prev, b)
+
+        t_run([0, 1])
         b1ps = psum.tile([P, 512], F32, name="mb", tag="mb")
         nc.tensor.transpose(b1ps[:, 0:P], b1z[:].bitcast(F32), ident[:])
-        nc.vector.tensor_copy(out=b1col[:], in_=b1ps[:, 0:16].bitcast(BF16))
+        b2ps = []
         for n in range(2):
-            b2ps = psum.tile([P, 512], F32, name="mb", tag="mb")
+            b2ps.append(psum.tile([P, 512], F32, name="mb", tag="mb"))
             nc.tensor.matmul(
-                out=b2ps[:], lhsT=ones[:], rhs=b2z[:, n * 512 : (n + 1) * 512],
+                out=b2ps[n][:], lhsT=ones[:], rhs=b2z[:, n * 512 : (n + 1) * 512],
                 start=True, stop=True,
             )
-            nc.scalar.copy(out=b2bc[:, n * 512 : (n + 1) * 512], in_=b2ps[:])
-        quant(0)
-        transposes(1)
-        next_load(1)
-        evac(1, 0, "V")
-        evac(1, 1, "S")
-        evac(1, 2, "V")
-        evac(1, 3, "S")
-        quant(1)
+        for s in range(3):
+            evac_quant(1, s)
+        nc.vector.tensor_copy(out=b1col[:], in_=b1ps[:, 0:16].bitcast(BF16))
+        evac_quant(1, 3)
+        for n in range(2):
+            nc.scalar.copy(out=b2bc[:, n * 512 : (n + 1) * 512], in_=b2ps[n][:])
+        m_run([0])
 
-        for p in range(18):
-            k = p + 2
-            if k < N_UNITS:
-                transposes(k)
-                next_load(k)
-            if p < 8:
-                mm1(p)
-            else:
-                mm2(*divmod(p - 8, 5))
-            if k < N_UNITS:
-                evac(k, 0, "V")
-                evac(k, 1, "S")
-                evac(k, 2, "S")
-                evac(k, 3, "S")
-            if 1 <= p <= 8:
-                regroup(p - 1)
-            if 2 <= p <= 9:
-                quant_h(p - 2)
-            if k < N_UNITS:
-                quant(k)
-            if p < 8:
-                for t in range(4):
-                    relu(p, t, "V" if (t == 3 and p % 2 == 1) else "S")
-            if p == 12 or p == 17:
-                for bt in range(4):
-                    finish((p - 8) // 5, bt)
+        def block(units, ps):
+            last = t_run(units)
+            for s in range(4):
+                evac_quant(last, s)
+            m_run(ps)
+
+        block([2, 3], [1])
+        for i in range(1, 8):
+            block([2 * i + 2, 2 * i + 3], [2 * i, 2 * i + 1])
+        block([18], [16, 17])

@@ -15,7 +15,10 @@ P = 128
 B, D_IN, HID, OUT = 512, 1024, 4096, 1024
 FLOPS = 2 * B * (D_IN * HID + (D_IN + HID) * OUT)
 
-RAW_BUFS = 8
+MANUAL = True
+RAW_BUFS = 6
+DV_UNITS = (15, 17, 18)
+SLOW_PER_UNIT = 4
 N_UNITS = 19
 
 
@@ -25,12 +28,14 @@ def tile_dpn_kernel(tc, x, W1, b1, W2, b2, out):
         const = ctx.enter_context(tc.tile_pool(name="const", bufs=1))
         keep = ctx.enter_context(tc.tile_pool(name="keep", bufs=1))
         rawp = ctx.enter_context(tc.tile_pool(name="rawp", bufs=RAW_BUFS))
+        rawdp = ctx.enter_context(tc.tile_pool(name="rawdp", bufs=3))
         grpp = ctx.enter_context(tc.tile_pool(name="grpp", bufs=3))
-        w1p = ctx.enter_context(tc.tile_pool(name="w1p", bufs=4))
+        w1p = ctx.enter_context(tc.tile_pool(name="w1p", bufs=3))
         hpp = ctx.enter_context(tc.tile_pool(name="hpp", bufs=3))
         ostp = ctx.enter_context(tc.tile_pool(name="ostp", bufs=4))
         psum = ctx.enter_context(tc.psum_pool(name="psum", bufs=4))
-        ctx.enter_context(tc.manual_schedule())
+        if MANUAL:
+            ctx.enter_context(tc.manual_schedule())
 
         xc = keep.tile([P, 1024], U32, name="xc", align_bytes=64)
         xs = keep.tile([P, 1024], U8, name="xs", align_bytes=64)
@@ -49,108 +54,120 @@ def tile_dpn_kernel(tc, x, W1, b1, W2, b2, out):
                 w2s[:, q * 1024 : (q + 1) * 1024],
             )
 
-        def is_w1(k):
-            return 1 <= k < 9
-
         def load(k):
             raw = rawp.tile([P, 4096], BF16, name="raw", tag="raw")
             raws[k] = raw
-            dst = raw[:].rearrange("p (s k) -> p s k", s=4)
             if k == 0:
                 src = x.rearrange("(s p) k -> p s k", p=P)
-                for s in range(4):
-                    nc.sync.dma_start(out=dst[:, s, :], in_=src[:, s, :])
-            elif k == 1:
-                src = W1[0:512, :].rearrange("(u p e) k -> p u e k", u=2, e=2)
-                for s in range(4):
-                    nc.sync.dma_start(out=dst[:, s, :], in_=src[:, s // 2, s % 2, :])
+                dst = raw[:].rearrange("p (s k) -> p s k", s=4)
+                nc.sync.dma_start(out=dst[:, 0:2, :], in_=src[:, 0:2, :])
+                nc.sync.dma_start(out=dst[:, 2:4, :], in_=src[:, 2:4, :])
             elif k < 9:
                 j = k - 1
                 src = W1[512 * j : 512 * (j + 1), :].rearrange(
                     "(u p e) k -> p u (e k)", u=2, e=2
                 )
-                nc.sync.dma_start(
-                    out=raw[:].rearrange("p (u f) -> p u f", u=2), in_=src
-                )
+                dst = raw[:].rearrange("p (u f) -> p u f", u=2)
+                if k == 1:
+                    nc.sync.dma_start(out=dst[:, 0:1, :], in_=src[:, 0:1, :])
+                    nc.sync.dma_start(out=dst[:, 1:2, :], in_=src[:, 1:2, :])
+                else:
+                    nc.sync.dma_start(out=dst, in_=src)
             else:
                 n, c = divmod(k - 9, 5)
                 src = W2[
                     512 * n : 512 * (n + 1), 1024 * c : 1024 * (c + 1)
                 ].rearrange("(s p) k -> p s k", p=P)
+                dst = raw[:].rearrange("p (s k) -> p s k", s=4)
                 nc.sync.dma_start(out=dst, in_=src)
 
-        def start_unit(k):
-            banks[k] = []
-            grps[k] = grpp.tile([P, 4096], BF16, name="grp", tag="grp", align_bytes=64)
-            if is_w1(k):
-                w1c = w1p.tile([P, 1024], U32, name="w1c", tag="w1c", align_bytes=64)
-                w1s = w1p.tile([P, 1024], U8, name="w1s", tag="w1s", align_bytes=64)
-                codes[k] = (w1c[:], w1s[:])
+        def slow_piece(k, i):
+            if i == 0:
+                raws[k] = rawdp.tile([P, 4096], BF16, name="rawd", tag="rawd", align_bytes=64)
+            n, c = divmod(k - 9, 5)
+            a, u, g = i // 4, (i // 2) % 2, i % 2
+            col = 1024 * c + 512 * g + 256 * u + 64 * a
+            nc.sync.dma_start(
+                out=raws[k][32 * a + u : 32 * a + 32 : 2, g * 2048 : (g + 1) * 2048].rearrange(
+                    "p (h w) -> p h w", w=64
+                ),
+                in_=W2[512 * n : 512 * (n + 1), col : col + 64].rearrange(
+                    "(h p) w -> p h w", p=16
+                ),
+            )
 
-        def transposes(k, s):
+        def dv_transpose(k, g):
+            if g == 0:
+                grps[k] = grpp.tile([P, 4096], BF16, name="grp", tag="grp", align_bytes=64)
+            nc.vector.transpose(
+                out=grps[k][:].bitcast(F32)[:, g * 1024 : (g + 1) * 1024],
+                in_=raws[k][:].bitcast(F32)[:, g * 1024 : (g + 1) * 1024],
+            )
+
+        def dv_quant(k, g):
+            cd, sc = codes[k]
+            nc.vector.quantize_mx(
+                out=cd[:, g * 512 : (g + 1) * 512].bitcast(FP8X4),
+                scales=sc[:, g * 512 : (g + 1) * 512],
+                in_=grps[k][:, g * 2048 : (g + 1) * 2048],
+            )
+
+        def transposes(k):
             rw = raws[k][:].bitcast(F32)
-            bank = psum.tile([P, 512], F32, name="tb", tag="tb")
-            for q in range(4):
-                nc.tensor.transpose(
-                    bank[:, q * P : (q + 1) * P],
-                    rw[:, s * 512 + q * P : s * 512 + (q + 1) * P],
-                    ident[:],
-                )
-            banks[k].append(bank)
+            bl = []
+            for s in range(4):
+                bank = psum.tile([P, 512], F32, name="tb", tag="tb")
+                for q in range(4):
+                    nc.tensor.transpose(
+                        bank[:, q * P : (q + 1) * P],
+                        rw[:, s * 512 + q * P : s * 512 + (q + 1) * P],
+                        ident[:],
+                    )
+                bl.append(bank)
+            banks[k] = bl
+            grps[k] = grpp.tile([P, 4096], BF16, name="grp", tag="grp", align_bytes=64)
 
         def evac(k, s, eng):
-            gw = grps[k][:].bitcast(F32)
-            if is_w1(k):
-                dst = gw[:, s * 512 : (s + 1) * 512].rearrange(
-                    "p (g r u) -> p g r u", g=2, u=2
-                )
-            else:
-                dst = gw.rearrange("p (g s r u) -> p g s r u", g=2, s=4, u=2)[:, :, s]
+            dst = grps[k][:].bitcast(F32).rearrange(
+                "p (g s r u) -> p g s r u", g=2, s=4, u=2
+            )[:, :, s]
             src = banks[k][s][:].rearrange("p (g u r) -> p g r u", g=2, u=2)
             if eng == "V":
                 nc.vector.tensor_copy(out=dst, in_=src)
             else:
                 nc.scalar.copy(out=dst, in_=src)
 
-        def quant_cols(k, lo, hi):
+        def quant(k):
+            if 1 <= k < 9:
+                w1c = w1p.tile([P, 1024], U32, name="w1c", tag="w1c", align_bytes=64)
+                w1s = w1p.tile([P, 1024], U8, name="w1s", tag="w1s", align_bytes=64)
+                codes[k] = (w1c[:], w1s[:])
             cd, sc = codes[k]
-            nc.vector.quantize_mx(
-                out=cd[:, lo:hi].bitcast(FP8X4),
-                scales=sc[:, lo:hi],
-                in_=grps[k][:, 4 * lo : 4 * hi],
-            )
-
-        def quant(k, s_lo, s_hi):
-            if is_w1(k):
-                quant_cols(k, s_lo * 256, s_hi * 256)
-            elif s_hi - s_lo == 4:
-                quant_cols(k, 0, 1024)
-            else:
-                for g in range(2):
-                    quant_cols(k, g * 512 + s_lo * P, g * 512 + s_hi * P)
+            nc.vector.quantize_mx(out=cd.bitcast(FP8X4), scales=sc, in_=grps[k][:])
 
         accs = {}
         hps = {}
         hgs = {}
 
-        def mm1(j, t):
+        def mm1(j):
             cd, sc = codes[1 + j]
-            if t == 0:
-                accs[j] = []
-                hps[j] = hpp.tile([P, 2048], BF16, name="hp", tag="hp", bufs=5)
-            acc = psum.tile([P, 512], F32, name="mb", tag="mb")
-            for g in range(2):
-                cols = slice(t * 256 + g * P, t * 256 + (g + 1) * P)
-                nc.tensor.matmul_mx(
-                    out=acc[:],
-                    lhsT=cd[:, cols].bitcast(FP8X4),
-                    lhsT_scale=sc[:, cols],
-                    rhs=xc[:, g * 512 : (g + 1) * 512].bitcast(FP8X4),
-                    rhs_scale=xs[:, g * 512 : (g + 1) * 512],
-                    start=(g == 0),
-                    stop=(g == 1),
-                )
-            accs[j].append(acc)
+            al = []
+            for t in range(4):
+                acc = psum.tile([P, 512], F32, name="mb", tag="mb")
+                for g in range(2):
+                    cols = slice(g * 512 + t * P, g * 512 + (t + 1) * P)
+                    nc.tensor.matmul_mx(
+                        out=acc[:],
+                        lhsT=cd[:, cols].bitcast(FP8X4),
+                        lhsT_scale=sc[:, cols],
+                        rhs=xc[:, g * 512 : (g + 1) * 512].bitcast(FP8X4),
+                        rhs_scale=xs[:, g * 512 : (g + 1) * 512],
+                        start=(g == 0),
+                        stop=(g == 1),
+                    )
+                al.append(acc)
+            accs[j] = al
+            hps[j] = hpp.tile([P, 2048], BF16, name="hp", tag="hp")
 
         def relu(j, t, eng):
             dst = hps[j][:, t * 512 : (t + 1) * 512]
@@ -182,27 +199,28 @@ def tile_dpn_kernel(tc, x, W1, b1, W2, b2, out):
 
         acc2 = {}
 
-        def mm2(n, c, bt):
+        def mm2(n, c):
             if c == 0:
-                if bt == 0:
-                    acc2[n] = []
-                acc2[n].append(psum.tile([P, 512], F32, name="mb", tag="mb"))
-            for gg in (2 * c, 2 * c + 1):
-                if gg < 2:
-                    lc, ls, base = xc, xs, gg * 512
-                else:
-                    lc, ls, base = hc, hs, (gg - 2) * 512
-                cols = slice(base + bt * P, base + (bt + 1) * P)
-                rcols = slice(n * 5120 + gg * 512, n * 5120 + (gg + 1) * 512)
-                nc.tensor.matmul_mx(
-                    out=acc2[n][bt][:],
-                    lhsT=lc[:, cols].bitcast(FP8X4),
-                    lhsT_scale=ls[:, cols],
-                    rhs=w2c[:, rcols].bitcast(FP8X4),
-                    rhs_scale=w2s[:, rcols],
-                    start=(gg == 0),
-                    stop=(gg == 9),
-                )
+                acc2[n] = [
+                    psum.tile([P, 512], F32, name="mb", tag="mb") for bt in range(4)
+                ]
+            for bt in range(4):
+                for gg in (2 * c, 2 * c + 1):
+                    if gg < 2:
+                        lc, ls, base = xc, xs, gg * 512
+                    else:
+                        lc, ls, base = hc, hs, (gg - 2) * 512
+                    cols = slice(base + bt * P, base + (bt + 1) * P)
+                    rcols = slice(n * 5120 + gg * 512, n * 5120 + (gg + 1) * 512)
+                    nc.tensor.matmul_mx(
+                        out=acc2[n][bt][:],
+                        lhsT=lc[:, cols].bitcast(FP8X4),
+                        lhsT_scale=ls[:, cols],
+                        rhs=w2c[:, rcols].bitcast(FP8X4),
+                        rhs_scale=w2s[:, rcols],
+                        start=(gg == 0),
+                        stop=(gg == 9),
+                    )
 
         def finish(n, bt):
             ost = ostp.tile([P, 512], F32, name="ost", tag="ost")
@@ -227,96 +245,96 @@ def tile_dpn_kernel(tc, x, W1, b1, W2, b2, out):
         nc.scalar.dma_start(out=b2z[0:1, :], in_=b2.rearrange("(o n) -> o n", o=1))
         make_identity(nc, ident[:])
 
-        for k in range(RAW_BUFS):
-            load(k)
+        normal = [k for k in range(N_UNITS) if k not in DV_UNITS]
+        slow = [(k, i) for k in DV_UNITS for i in range(16)]
+        issued = {"normal": 0, "slow": 0}
 
-        def evac_pattern(k):
-            if k < 2 or (k < 10 and k % 2 == 0):
-                return "VSVS"
-            return "SSVS"
+        def next_load():
+            if issued["normal"] < len(normal):
+                load(normal[issued["normal"]])
+                issued["normal"] += 1
 
-        def quant_parts(k):
-            if k < 2:
-                return 1
-            if k < 9:
-                return 2
-            return 4
+        def next_slow():
+            for r in range(SLOW_PER_UNIT):
+                if issued["slow"] < len(slow):
+                    slow_piece(*slow[issued["slow"]])
+                    issued["slow"] += 1
 
-        def evac_quant(k, s):
-            evac(k, s, evac_pattern(k)[s])
-            step = quant_parts(k)
-            if (s + 1) % step == 0:
-                quant(k, s + 1 - step, s + 1)
+        for r in range(RAW_BUFS):
+            next_load()
 
-        def t_run(units):
-            prev = None
-            for k in units:
-                start_unit(k)
-                for s in range(4):
-                    if prev is not None:
-                        evac_quant(prev, s)
-                    transposes(k, s)
-                if k + RAW_BUFS < N_UNITS:
-                    load(k + RAW_BUFS)
-                prev = k
-            return prev
-
-        def drain(p, b):
-            if p < 8:
-                relu(p, b, "V" if (b == 3 and p % 2 == 0) else "S")
-            if p == 12 or p == 17:
-                finish((p - 8) // 5, b)
-            if b == 3:
-                if 2 <= p <= 7:
-                    quant_h(p - 2)
-                if 1 <= p <= 6:
-                    regroup(p - 1)
-                if p == 9:
-                    regroup(6)
-                    regroup(7)
-                    quant_h(6)
-                    quant_h(7)
-
-        def m_run(ps):
-            prev = None
-            for p in ps:
-                for b in range(4):
-                    if prev is not None:
-                        drain(prev, b)
-                    if p < 8:
-                        mm1(p, b)
-                    else:
-                        n, c = divmod(p - 8, 5)
-                        mm2(n, c, b)
-                prev = p
-            for b in range(4):
-                drain(prev, b)
-
-        t_run([0, 1])
+        transposes(0)
+        next_load()
+        next_slow()
+        evac(0, 0, "V")
+        evac(0, 1, "S")
+        evac(0, 2, "V")
+        evac(0, 3, "S")
         b1ps = psum.tile([P, 512], F32, name="mb", tag="mb")
         nc.tensor.transpose(b1ps[:, 0:P], b1z[:].bitcast(F32), ident[:])
-        b2ps = []
+        nc.vector.tensor_copy(out=b1col[:], in_=b1ps[:, 0:16].bitcast(BF16))
         for n in range(2):
-            b2ps.append(psum.tile([P, 512], F32, name="mb", tag="mb"))
+            b2ps = psum.tile([P, 512], F32, name="mb", tag="mb")
             nc.tensor.matmul(
-                out=b2ps[n][:], lhsT=ones[:], rhs=b2z[:, n * 512 : (n + 1) * 512],
+                out=b2ps[:], lhsT=ones[:], rhs=b2z[:, n * 512 : (n + 1) * 512],
                 start=True, stop=True,
             )
-        for s in range(3):
-            evac_quant(1, s)
-        nc.vector.tensor_copy(out=b1col[:], in_=b1ps[:, 0:16].bitcast(BF16))
-        evac_quant(1, 3)
-        for n in range(2):
-            nc.scalar.copy(out=b2bc[:, n * 512 : (n + 1) * 512], in_=b2ps[n][:])
-        m_run([0])
+            nc.scalar.copy(out=b2bc[:, n * 512 : (n + 1) * 512], in_=b2ps[:])
+        quant(0)
+        transposes(1)
+        next_load()
+        next_slow()
+        evac(1, 0, "V")
+        evac(1, 1, "S")
+        evac(1, 2, "V")
+        evac(1, 3, "S")
+        quant(1)
 
-        def block(units, ps):
-            last = t_run(units)
-            for s in range(4):
-                evac_quant(last, s)
-            m_run(ps)
+        dv_after = {
+            8: [("T", 15, 0)],
+            9: [("Q", 15, 0), ("T", 15, 1)],
+            10: [("Q", 15, 1), ("T", 17, 0)],
+            11: [("Q", 17, 0), ("T", 17, 1)],
+            12: [("Q", 17, 1)],
+            13: [("T", 18, 0), ("T", 18, 1), ("Q", 18, 0)],
+            14: [("Q", 18, 1)],
+        }
 
-        block([2, 3], [1])
-        for i in range(1, 8):
-            block([2 * i + 2, 2 * i + 3], [2 * i, 2 * i + 1])
-        block([18], [16, 17])
+        for p in range(18):
+            k = normal[p + 2] if p + 2 < len(normal) else None
+            if k is not None:
+                transposes(k)
+                next_load()
+                next_slow()
+            if p < 8:
+                mm1(p)
+            else:
+                mm2(*divmod(p - 8, 5))
+            if k is not None:
+                evac(k, 0, "V" if k < 10 else "S")
+                evac(k, 1, "S")
+                evac(k, 2, "S")
+                evac(k, 3, "S")
+            if 1 <= p <= 8:
+                regroup(p - 1)
+            if 2 <= p <= 9:
+                quant_h(p - 2)
+            if p == 12:
+                finish(0, 0)
+                finish(0, 1)
+            if k is not None:
+                quant(k)
+            if p == 12:
+                finish(0, 2)
+                finish(0, 3)
+            for what, kd, g in dv_after.get(p, []):
+                if what == "T":
+                    dv_transpose(kd, g)
+                else:
+                    dv_quant(kd, g)
+            if p < 8:
+                for t in range(4):
+                    relu(p, t, "V" if (t == 3 and p % 2 == 1) else "S")
+            if p == 17:
+                for bt in range(4):
+                    finish(1, bt)

@@ -15,10 +15,7 @@ P = 128
 B, D_IN, HID, OUT = 512, 1024, 4096, 1024
 FLOPS = 2 * B * (D_IN * HID + (D_IN + HID) * OUT)
 
-MANUAL = True
-RAW_BUFS = 6
-DV_UNITS = (15, 17, 18)
-SLOW_PER_UNIT = 4
+RAW_BUFS = 8
 N_UNITS = 19
 
 
@@ -28,14 +25,12 @@ def tile_dpn_kernel(tc, x, W1, b1, W2, b2, out):
         const = ctx.enter_context(tc.tile_pool(name="const", bufs=1))
         keep = ctx.enter_context(tc.tile_pool(name="keep", bufs=1))
         rawp = ctx.enter_context(tc.tile_pool(name="rawp", bufs=RAW_BUFS))
-        rawdp = ctx.enter_context(tc.tile_pool(name="rawdp", bufs=3))
         grpp = ctx.enter_context(tc.tile_pool(name="grpp", bufs=3))
-        w1p = ctx.enter_context(tc.tile_pool(name="w1p", bufs=3))
+        w1p = ctx.enter_context(tc.tile_pool(name="w1p", bufs=4))
         hpp = ctx.enter_context(tc.tile_pool(name="hpp", bufs=3))
         ostp = ctx.enter_context(tc.tile_pool(name="ostp", bufs=4))
         psum = ctx.enter_context(tc.psum_pool(name="psum", bufs=4))
-        if MANUAL:
-            ctx.enter_context(tc.manual_schedule())
+        ctx.enter_context(tc.manual_schedule())
 
         xc = keep.tile([P, 1024], U32, name="xc", align_bytes=64)
         xs = keep.tile([P, 1024], U8, name="xs", align_bytes=64)
@@ -54,120 +49,108 @@ def tile_dpn_kernel(tc, x, W1, b1, W2, b2, out):
                 w2s[:, q * 1024 : (q + 1) * 1024],
             )
 
+        def is_w1(k):
+            return 1 <= k < 9
+
         def load(k):
             raw = rawp.tile([P, 4096], BF16, name="raw", tag="raw")
             raws[k] = raw
+            dst = raw[:].rearrange("p (s k) -> p s k", s=4)
             if k == 0:
                 src = x.rearrange("(s p) k -> p s k", p=P)
-                dst = raw[:].rearrange("p (s k) -> p s k", s=4)
-                nc.sync.dma_start(out=dst[:, 0:2, :], in_=src[:, 0:2, :])
-                nc.sync.dma_start(out=dst[:, 2:4, :], in_=src[:, 2:4, :])
+                for s in range(4):
+                    nc.sync.dma_start(out=dst[:, s, :], in_=src[:, s, :])
+            elif k == 1:
+                src = W1[0:512, :].rearrange("(u p e) k -> p u e k", u=2, e=2)
+                for s in range(4):
+                    nc.sync.dma_start(out=dst[:, s, :], in_=src[:, s // 2, s % 2, :])
             elif k < 9:
                 j = k - 1
                 src = W1[512 * j : 512 * (j + 1), :].rearrange(
                     "(u p e) k -> p u (e k)", u=2, e=2
                 )
-                dst = raw[:].rearrange("p (u f) -> p u f", u=2)
-                if k == 1:
-                    nc.sync.dma_start(out=dst[:, 0:1, :], in_=src[:, 0:1, :])
-                    nc.sync.dma_start(out=dst[:, 1:2, :], in_=src[:, 1:2, :])
-                else:
-                    nc.sync.dma_start(out=dst, in_=src)
+                nc.sync.dma_start(
+                    out=raw[:].rearrange("p (u f) -> p u f", u=2), in_=src
+                )
             else:
                 n, c = divmod(k - 9, 5)
                 src = W2[
                     512 * n : 512 * (n + 1), 1024 * c : 1024 * (c + 1)
                 ].rearrange("(s p) k -> p s k", p=P)
-                dst = raw[:].rearrange("p (s k) -> p s k", s=4)
                 nc.sync.dma_start(out=dst, in_=src)
 
-        def slow_piece(k, i):
-            if i == 0:
-                raws[k] = rawdp.tile([P, 4096], BF16, name="rawd", tag="rawd", align_bytes=64)
-            n, c = divmod(k - 9, 5)
-            a, u, g = i // 4, (i // 2) % 2, i % 2
-            col = 1024 * c + 512 * g + 256 * u + 64 * a
-            nc.sync.dma_start(
-                out=raws[k][32 * a + u : 32 * a + 32 : 2, g * 2048 : (g + 1) * 2048].rearrange(
-                    "p (h w) -> p h w", w=64
-                ),
-                in_=W2[512 * n : 512 * (n + 1), col : col + 64].rearrange(
-                    "(h p) w -> p h w", p=16
-                ),
-            )
-
-        def dv_transpose(k, g):
-            if g == 0:
-                grps[k] = grpp.tile([P, 4096], BF16, name="grp", tag="grp", align_bytes=64)
-            nc.vector.transpose(
-                out=grps[k][:].bitcast(F32)[:, g * 1024 : (g + 1) * 1024],
-                in_=raws[k][:].bitcast(F32)[:, g * 1024 : (g + 1) * 1024],
-            )
-
-        def dv_quant(k, g):
-            cd, sc = codes[k]
-            nc.vector.quantize_mx(
-                out=cd[:, g * 512 : (g + 1) * 512].bitcast(FP8X4),
-                scales=sc[:, g * 512 : (g + 1) * 512],
-                in_=grps[k][:, g * 2048 : (g + 1) * 2048],
-            )
-
-        def transposes(k):
-            rw = raws[k][:].bitcast(F32)
-            bl = []
-            for s in range(4):
-                bank = psum.tile([P, 512], F32, name="tb", tag="tb")
-                for q in range(4):
-                    nc.tensor.transpose(
-                        bank[:, q * P : (q + 1) * P],
-                        rw[:, s * 512 + q * P : s * 512 + (q + 1) * P],
-                        ident[:],
-                    )
-                bl.append(bank)
-            banks[k] = bl
+        def start_unit(k):
+            banks[k] = []
             grps[k] = grpp.tile([P, 4096], BF16, name="grp", tag="grp", align_bytes=64)
+            if is_w1(k):
+                w1c = w1p.tile([P, 1024], U32, name="w1c", tag="w1c", align_bytes=64)
+                w1s = w1p.tile([P, 1024], U8, name="w1s", tag="w1s", align_bytes=64)
+                codes[k] = (w1c[:], w1s[:])
+
+        def transposes(k, s):
+            rw = raws[k][:].bitcast(F32)
+            bank = psum.tile([P, 512], F32, name="tb", tag="tb")
+            for q in range(4):
+                nc.tensor.transpose(
+                    bank[:, q * P : (q + 1) * P],
+                    rw[:, s * 512 + q * P : s * 512 + (q + 1) * P],
+                    ident[:],
+                )
+            banks[k].append(bank)
 
         def evac(k, s, eng):
-            dst = grps[k][:].bitcast(F32).rearrange(
-                "p (g s r u) -> p g s r u", g=2, s=4, u=2
-            )[:, :, s]
+            gw = grps[k][:].bitcast(F32)
+            if is_w1(k):
+                dst = gw[:, s * 512 : (s + 1) * 512].rearrange(
+                    "p (g r u) -> p g r u", g=2, u=2
+                )
+            else:
+                dst = gw.rearrange("p (g s r u) -> p g s r u", g=2, s=4, u=2)[:, :, s]
             src = banks[k][s][:].rearrange("p (g u r) -> p g r u", g=2, u=2)
             if eng == "V":
                 nc.vector.tensor_copy(out=dst, in_=src)
             else:
                 nc.scalar.copy(out=dst, in_=src)
 
-        def quant(k):
-            if 1 <= k < 9:
-                w1c = w1p.tile([P, 1024], U32, name="w1c", tag="w1c", align_bytes=64)
-                w1s = w1p.tile([P, 1024], U8, name="w1s", tag="w1s", align_bytes=64)
-                codes[k] = (w1c[:], w1s[:])
+        def quant_cols(k, lo, hi):
             cd, sc = codes[k]
-            nc.vector.quantize_mx(out=cd.bitcast(FP8X4), scales=sc, in_=grps[k][:])
+            nc.vector.quantize_mx(
+                out=cd[:, lo:hi].bitcast(FP8X4),
+                scales=sc[:, lo:hi],
+                in_=grps[k][:, 4 * lo : 4 * hi],
+            )
+
+        def quant(k, s_lo, s_hi):
+            if is_w1(k):
+                quant_cols(k, s_lo * 256, s_hi * 256)
+            elif s_hi - s_lo == 4:
+                quant_cols(k, 0, 1024)
+            else:
+                for g in range(2):
+                    quant_cols(k, g * 512 + s_lo * P, g * 512 + s_hi * P)
 
         accs = {}
         hps = {}
         hgs = {}
 
-        def mm1(j):
+        def mm1(j, t):
             cd, sc = codes[1 + j]
-            al = []
-            for t in range(4):
-                acc = psum.tile([P, 512], F32, name="mb", tag="mb")
-                for g in range(2):
-                    cols = slice(g * 512 + t * P, g * 512 + (t + 1) * P)
-                    nc.tensor.matmul_mx(
-                        out=acc[:],
-                        lhsT=cd[:, cols].bitcast(FP8X4),
-                        lhsT_scale=sc[:, cols],
-                        rhs=xc[:, g * 512 : (g + 1) * 512].bitcast(FP8X4),
-                        rhs_scale=xs[:, g * 512 : (g + 1) * 512],
-                        start=(g == 0),
-                        stop=(g == 1),
-                    )
-                al.append(acc)
-            accs[j] = al
-            hps[j] = hpp.tile([P, 2048], BF16, name="hp", tag="hp")
+            if t == 0:
+                accs[j] = []
+                hps[j] = hpp.tile([P, 2048], BF16, name="hp", tag="hp", bufs=4)
+            acc = psum.tile([P, 512], F32, name="mb", tag="mb")
+            for g in range(2):
+                cols = slice(t * 256 + g * P, t * 256 + (g + 1) * P)
+                nc.tensor.matmul_mx(
+                    out=acc[:],
+                    lhsT=cd[:, cols].bitcast(FP8X4),
+                    lhsT_scale=sc[:, cols],
+                    rhs=xc[:, g * 512 : (g + 1) * 512].bitcast(FP8X4),
+                    rhs_scale=xs[:, g * 512 : (g + 1) * 512],
+                    start=(g == 0),
+                    stop=(g == 1),
+                )
+            accs[j].append(acc)
 
         def relu(j, t, eng):
             dst = hps[j][:, t * 512 : (t + 1) * 512]
@@ -199,38 +182,41 @@ def tile_dpn_kernel(tc, x, W1, b1, W2, b2, out):
 
         acc2 = {}
 
-        def mm2(n, c):
+        def mm2(n, c, bt):
             if c == 0:
-                acc2[n] = [
-                    psum.tile([P, 512], F32, name="mb", tag="mb") for bt in range(4)
-                ]
-            for bt in range(4):
-                for gg in (2 * c, 2 * c + 1):
-                    if gg < 2:
-                        lc, ls, base = xc, xs, gg * 512
-                    else:
-                        lc, ls, base = hc, hs, (gg - 2) * 512
-                    cols = slice(base + bt * P, base + (bt + 1) * P)
-                    rcols = slice(n * 5120 + gg * 512, n * 5120 + (gg + 1) * 512)
-                    nc.tensor.matmul_mx(
-                        out=acc2[n][bt][:],
-                        lhsT=lc[:, cols].bitcast(FP8X4),
-                        lhsT_scale=ls[:, cols],
-                        rhs=w2c[:, rcols].bitcast(FP8X4),
-                        rhs_scale=w2s[:, rcols],
-                        start=(gg == 0),
-                        stop=(gg == 9),
-                    )
+                if bt == 0:
+                    acc2[n] = []
+                acc2[n].append(psum.tile([P, 512], F32, name="mb", tag="mb"))
+            for gg in (2 * c, 2 * c + 1):
+                if gg < 2:
+                    lc, ls, base = xc, xs, gg * 512
+                else:
+                    lc, ls, base = hc, hs, (gg - 2) * 512
+                cols = slice(base + bt * P, base + (bt + 1) * P)
+                rcols = slice(n * 5120 + gg * 512, n * 5120 + (gg + 1) * 512)
+                nc.tensor.matmul_mx(
+                    out=acc2[n][bt][:],
+                    lhsT=lc[:, cols].bitcast(FP8X4),
+                    lhsT_scale=ls[:, cols],
+                    rhs=w2c[:, rcols].bitcast(FP8X4),
+                    rhs_scale=w2s[:, rcols],
+                    start=(gg == 0),
+                    stop=(gg == 9),
+                )
 
-        def finish(n, bt):
+        def finish(n, bt, parts):
             ost = ostp.tile([P, 512], F32, name="ost", tag="ost")
-            nc.vector.tensor_tensor(
-                out=ost[:], in0=acc2[n][bt][:], in1=b2bc[:, n * 512 : (n + 1) * 512],
-                op=ALU.add,
-            )
-            nc.sync.dma_start(
-                out=out[bt * P : (bt + 1) * P, n * 512 : (n + 1) * 512], in_=ost[:]
-            )
+            step = 512 // parts
+            for lo in range(0, 512, step):
+                hi = lo + step
+                nc.vector.tensor_tensor(
+                    out=ost[:, lo:hi], in0=acc2[n][bt][:, lo:hi],
+                    in1=b2bc[:, n * 512 + lo : n * 512 + hi], op=ALU.add,
+                )
+                nc.sync.dma_start(
+                    out=out[bt * P : (bt + 1) * P, n * 512 + lo : n * 512 + hi],
+                    in_=ost[:, lo:hi],
+                )
 
         b1z = const.tile([P, 256], BF16, name="b1z")
         b2z = const.tile([P, OUT], BF16, name="b2z")
@@ -245,96 +231,93 @@ def tile_dpn_kernel(tc, x, W1, b1, W2, b2, out):
         nc.scalar.dma_start(out=b2z[0:1, :], in_=b2.rearrange("(o n) -> o n", o=1))
         make_identity(nc, ident[:])
 
-        normal = [k for k in range(N_UNITS) if k not in DV_UNITS]
-        slow = [(k, i) for k in DV_UNITS for i in range(16)]
-        issued = {"normal": 0, "slow": 0}
+        for k in range(RAW_BUFS):
+            load(k)
 
-        def next_load():
-            if issued["normal"] < len(normal):
-                load(normal[issued["normal"]])
-                issued["normal"] += 1
+        g_at = (1, 2, 4, 5, 7, 8, 10, 10)
+        qh_at = (2, 3, 5, 6, 8, 9, 11, 11)
 
-        def next_slow():
-            for r in range(SLOW_PER_UNIT):
-                if issued["slow"] < len(slow):
-                    slow_piece(*slow[issued["slow"]])
-                    issued["slow"] += 1
+        def evac_pattern(k):
+            if k < 2 or k == 18:
+                return "VSVS"
+            return "VSSS"
 
-        for r in range(RAW_BUFS):
-            next_load()
+        def t_unit(k, before_bank):
+            start_unit(k)
+            for s in range(4):
+                before_bank(s)
+                transposes(k, s)
+            if k + RAW_BUFS < N_UNITS:
+                load(k + RAW_BUFS)
 
-        transposes(0)
-        next_load()
-        next_slow()
-        evac(0, 0, "V")
-        evac(0, 1, "S")
-        evac(0, 2, "V")
-        evac(0, 3, "S")
+        def nothing(s):
+            return None
+
+        def evac_quant_piece(k, s):
+            evac(k, s, evac_pattern(k)[s])
+            quant(k, s, s + 1)
+
+        t_unit(0, nothing)
+        t_unit(1, lambda s: evac_quant_piece(0, s))
         b1ps = psum.tile([P, 512], F32, name="mb", tag="mb")
         nc.tensor.transpose(b1ps[:, 0:P], b1z[:].bitcast(F32), ident[:])
-        nc.vector.tensor_copy(out=b1col[:], in_=b1ps[:, 0:16].bitcast(BF16))
+        b2ps = []
         for n in range(2):
-            b2ps = psum.tile([P, 512], F32, name="mb", tag="mb")
+            b2ps.append(psum.tile([P, 512], F32, name="mb", tag="mb"))
             nc.tensor.matmul(
-                out=b2ps[:], lhsT=ones[:], rhs=b2z[:, n * 512 : (n + 1) * 512],
+                out=b2ps[n][:], lhsT=ones[:], rhs=b2z[:, n * 512 : (n + 1) * 512],
                 start=True, stop=True,
             )
-            nc.scalar.copy(out=b2bc[:, n * 512 : (n + 1) * 512], in_=b2ps[:])
-        quant(0)
-        transposes(1)
-        next_load()
-        next_slow()
-        evac(1, 0, "V")
-        evac(1, 1, "S")
-        evac(1, 2, "V")
-        evac(1, 3, "S")
-        quant(1)
+        for s in range(3):
+            evac_quant_piece(1, s)
+        nc.vector.tensor_copy(out=b1col[:], in_=b1ps[:, 0:16].bitcast(BF16))
+        evac_quant_piece(1, 3)
+        for n in range(2):
+            nc.scalar.copy(out=b2bc[:, n * 512 : (n + 1) * 512], in_=b2ps[n][:])
+        mm1(0, 0)
+        mm1(0, 1)
+        relu(0, 0, "S")
+        relu(0, 1, "S")
+        t_unit(2, nothing)
+        mm1(0, 2)
+        mm1(0, 3)
+        for s in range(4):
+            evac(2, s, evac_pattern(2)[s])
+        quant(2, 0, 4)
+        relu(0, 2, "S")
+        relu(0, 3, "V")
 
-        dv_after = {
-            8: [("T", 15, 0)],
-            9: [("Q", 15, 0), ("T", 15, 1)],
-            10: [("Q", 15, 1), ("T", 17, 0)],
-            11: [("Q", 17, 0), ("T", 17, 1)],
-            12: [("Q", 17, 1)],
-            13: [("T", 18, 0), ("T", 18, 1), ("Q", 18, 0)],
-            14: [("Q", 18, 1)],
-        }
-
-        for p in range(18):
-            k = normal[p + 2] if p + 2 < len(normal) else None
-            if k is not None:
-                transposes(k)
-                next_load()
-                next_slow()
-            if p < 8:
-                mm1(p)
-            else:
-                mm2(*divmod(p - 8, 5))
-            if k is not None:
-                evac(k, 0, "V" if k < 10 else "S")
-                evac(k, 1, "S")
-                evac(k, 2, "S")
-                evac(k, 3, "S")
-            if 1 <= p <= 8:
-                regroup(p - 1)
-            if 2 <= p <= 9:
-                quant_h(p - 2)
-            if p == 12:
-                finish(0, 0)
-                finish(0, 1)
-            if k is not None:
-                quant(k)
-            if p == 12:
-                finish(0, 2)
-                finish(0, 3)
-            for what, kd, g in dv_after.get(p, []):
-                if what == "T":
-                    dv_transpose(kd, g)
+        for p in range(1, 18):
+            k = p + 2
+            if k < N_UNITS:
+                t_unit(k, nothing)
+            for b in range(4):
+                if p < 8:
+                    mm1(p, b)
                 else:
-                    dv_quant(kd, g)
+                    n, c = divmod(p - 8, 5)
+                    mm2(n, c, b)
+            if k < N_UNITS:
+                for s in range(4):
+                    evac(k, s, evac_pattern(k)[s])
+            for j in range(8):
+                if g_at[j] == p:
+                    regroup(j)
+            for j in range(8):
+                if qh_at[j] == p:
+                    quant_h(j)
+            if p == 12:
+                finish(0, 0, 1)
+                finish(0, 1, 1)
+            if k < N_UNITS:
+                quant(k, 0, 4)
+            if p == 12:
+                finish(0, 2, 1)
+                finish(0, 3, 1)
             if p < 8:
                 for t in range(4):
-                    relu(p, t, "V" if (t == 3 and p % 2 == 1) else "S")
+                    relu(p, t, "V" if t == 3 else "S")
             if p == 17:
-                for bt in range(4):
-                    finish(1, bt)
+                for bt in range(3):
+                    finish(1, bt, 1)
+                finish(1, 3, 2)

@@ -15,7 +15,10 @@ P = 128
 B, D_IN, HID, OUT = 512, 1024, 4096, 1024
 FLOPS = 2 * B * (D_IN * HID + (D_IN + HID) * OUT)
 
-RAW_BUFS = 8
+MANUAL = True
+RAW_BUFS = 9
+DV_UNITS = (17,)
+LOAD_ORDER = tuple(range(17)) + (18, 17)
 N_UNITS = 19
 
 
@@ -26,11 +29,12 @@ def tile_dpn_kernel(tc, x, W1, b1, W2, b2, out):
         keep = ctx.enter_context(tc.tile_pool(name="keep", bufs=1))
         rawp = ctx.enter_context(tc.tile_pool(name="rawp", bufs=RAW_BUFS))
         grpp = ctx.enter_context(tc.tile_pool(name="grpp", bufs=3))
-        w1p = ctx.enter_context(tc.tile_pool(name="w1p", bufs=4))
+        w1p = ctx.enter_context(tc.tile_pool(name="w1p", bufs=3))
         hpp = ctx.enter_context(tc.tile_pool(name="hpp", bufs=3))
         ostp = ctx.enter_context(tc.tile_pool(name="ostp", bufs=4))
         psum = ctx.enter_context(tc.psum_pool(name="psum", bufs=4))
-        ctx.enter_context(tc.manual_schedule())
+        if MANUAL:
+            ctx.enter_context(tc.manual_schedule())
 
         xc = keep.tile([P, 1024], U32, name="xc", align_bytes=64)
         xs = keep.tile([P, 1024], U8, name="xs", align_bytes=64)
@@ -49,108 +53,118 @@ def tile_dpn_kernel(tc, x, W1, b1, W2, b2, out):
                 w2s[:, q * 1024 : (q + 1) * 1024],
             )
 
-        def is_w1(k):
-            return 1 <= k < 9
-
         def load(k):
-            raw = rawp.tile([P, 4096], BF16, name="raw", tag="raw")
+            raw = rawp.tile([P, 4096], BF16, name="raw", tag="raw", align_bytes=64)
             raws[k] = raw
-            dst = raw[:].rearrange("p (s k) -> p s k", s=4)
-            if k == 0:
+            if k in DV_UNITS:
+                n, c = divmod(k - 9, 5)
+                for i in range(16):
+                    a, u, g = i // 4, (i // 2) % 2, i % 2
+                    col = 1024 * c + 512 * g + 256 * u + 64 * a
+                    nc.sync.dma_start(
+                        out=raw[
+                            32 * a + u : 32 * a + 32 : 2, g * 2048 : (g + 1) * 2048
+                        ].rearrange("p (h w) -> p h w", w=64),
+                        in_=W2[512 * n : 512 * (n + 1), col : col + 64].rearrange(
+                            "(h p) w -> p h w", p=16
+                        ),
+                    )
+            elif k == 0:
                 src = x.rearrange("(s p) k -> p s k", p=P)
-                for s in range(4):
-                    nc.sync.dma_start(out=dst[:, s, :], in_=src[:, s, :])
-            elif k == 1:
-                src = W1[0:512, :].rearrange("(u p e) k -> p u e k", u=2, e=2)
-                for s in range(4):
-                    nc.sync.dma_start(out=dst[:, s, :], in_=src[:, s // 2, s % 2, :])
+                dst = raw[:].rearrange("p (s k) -> p s k", s=4)
+                nc.sync.dma_start(out=dst[:, 0:2, :], in_=src[:, 0:2, :])
+                nc.sync.dma_start(out=dst[:, 2:4, :], in_=src[:, 2:4, :])
             elif k < 9:
                 j = k - 1
                 src = W1[512 * j : 512 * (j + 1), :].rearrange(
                     "(u p e) k -> p u (e k)", u=2, e=2
                 )
-                nc.sync.dma_start(
-                    out=raw[:].rearrange("p (u f) -> p u f", u=2), in_=src
-                )
+                dst = raw[:].rearrange("p (u f) -> p u f", u=2)
+                if k == 1:
+                    nc.sync.dma_start(out=dst[:, 0:1, :], in_=src[:, 0:1, :])
+                    nc.sync.dma_start(out=dst[:, 1:2, :], in_=src[:, 1:2, :])
+                else:
+                    nc.sync.dma_start(out=dst, in_=src)
             else:
                 n, c = divmod(k - 9, 5)
                 src = W2[
                     512 * n : 512 * (n + 1), 1024 * c : 1024 * (c + 1)
                 ].rearrange("(s p) k -> p s k", p=P)
+                dst = raw[:].rearrange("p (s k) -> p s k", s=4)
                 nc.sync.dma_start(out=dst, in_=src)
 
-        def start_unit(k):
-            banks[k] = []
-            grps[k] = grpp.tile([P, 4096], BF16, name="grp", tag="grp", align_bytes=64)
-            if is_w1(k):
-                w1c = w1p.tile([P, 1024], U32, name="w1c", tag="w1c", align_bytes=64)
-                w1s = w1p.tile([P, 1024], U8, name="w1s", tag="w1s", align_bytes=64)
-                codes[k] = (w1c[:], w1s[:])
+        def dv_transpose(k, g):
+            if g == 0:
+                grps[k] = grpp.tile([P, 4096], BF16, name="grp", tag="grp", align_bytes=64)
+            nc.vector.transpose(
+                out=grps[k][:].bitcast(F32)[:, g * 1024 : (g + 1) * 1024],
+                in_=raws[k][:].bitcast(F32)[:, g * 1024 : (g + 1) * 1024],
+            )
 
-        def transposes(k, s):
+        def dv_quant(k, g):
+            cd, sc = codes[k]
+            nc.vector.quantize_mx(
+                out=cd[:, g * 512 : (g + 1) * 512].bitcast(FP8X4),
+                scales=sc[:, g * 512 : (g + 1) * 512],
+                in_=grps[k][:, g * 2048 : (g + 1) * 2048],
+            )
+
+        def transposes(k):
             rw = raws[k][:].bitcast(F32)
-            bank = psum.tile([P, 512], F32, name="tb", tag="tb")
-            for q in range(4):
-                nc.tensor.transpose(
-                    bank[:, q * P : (q + 1) * P],
-                    rw[:, s * 512 + q * P : s * 512 + (q + 1) * P],
-                    ident[:],
-                )
-            banks[k].append(bank)
+            bl = []
+            for s in range(4):
+                bank = psum.tile([P, 512], F32, name="tb", tag="tb")
+                for q in range(4):
+                    nc.tensor.transpose(
+                        bank[:, q * P : (q + 1) * P],
+                        rw[:, s * 512 + q * P : s * 512 + (q + 1) * P],
+                        ident[:],
+                    )
+                bl.append(bank)
+            banks[k] = bl
+            grps[k] = grpp.tile([P, 4096], BF16, name="grp", tag="grp", align_bytes=64)
 
         def evac(k, s, eng):
-            gw = grps[k][:].bitcast(F32)
-            if is_w1(k):
-                dst = gw[:, s * 512 : (s + 1) * 512].rearrange(
-                    "p (g r u) -> p g r u", g=2, u=2
-                )
-            else:
-                dst = gw.rearrange("p (g s r u) -> p g s r u", g=2, s=4, u=2)[:, :, s]
+            dst = grps[k][:].bitcast(F32).rearrange(
+                "p (g s r u) -> p g s r u", g=2, s=4, u=2
+            )[:, :, s]
             src = banks[k][s][:].rearrange("p (g u r) -> p g r u", g=2, u=2)
             if eng == "V":
                 nc.vector.tensor_copy(out=dst, in_=src)
             else:
                 nc.scalar.copy(out=dst, in_=src)
 
-        def quant_cols(k, lo, hi):
+        def quant(k):
+            if 1 <= k < 9:
+                w1c = w1p.tile([P, 1024], U32, name="w1c", tag="w1c", align_bytes=64)
+                w1s = w1p.tile([P, 1024], U8, name="w1s", tag="w1s", align_bytes=64)
+                codes[k] = (w1c[:], w1s[:])
             cd, sc = codes[k]
-            nc.vector.quantize_mx(
-                out=cd[:, lo:hi].bitcast(FP8X4),
-                scales=sc[:, lo:hi],
-                in_=grps[k][:, 4 * lo : 4 * hi],
-            )
-
-        def quant(k, s_lo, s_hi):
-            if is_w1(k):
-                quant_cols(k, s_lo * 256, s_hi * 256)
-            elif s_hi - s_lo == 4:
-                quant_cols(k, 0, 1024)
-            else:
-                for g in range(2):
-                    quant_cols(k, g * 512 + s_lo * P, g * 512 + s_hi * P)
+            nc.vector.quantize_mx(out=cd.bitcast(FP8X4), scales=sc, in_=grps[k][:])
 
         accs = {}
         hps = {}
         hgs = {}
 
-        def mm1(j, t):
+        def mm1(j):
             cd, sc = codes[1 + j]
-            if t == 0:
-                accs[j] = []
-                hps[j] = hpp.tile([P, 2048], BF16, name="hp", tag="hp", bufs=4)
-            acc = psum.tile([P, 512], F32, name="mb", tag="mb")
-            for g in range(2):
-                cols = slice(t * 256 + g * P, t * 256 + (g + 1) * P)
-                nc.tensor.matmul_mx(
-                    out=acc[:],
-                    lhsT=cd[:, cols].bitcast(FP8X4),
-                    lhsT_scale=sc[:, cols],
-                    rhs=xc[:, g * 512 : (g + 1) * 512].bitcast(FP8X4),
-                    rhs_scale=xs[:, g * 512 : (g + 1) * 512],
-                    start=(g == 0),
-                    stop=(g == 1),
-                )
-            accs[j].append(acc)
+            al = []
+            for t in range(4):
+                acc = psum.tile([P, 512], F32, name="mb", tag="mb")
+                for g in range(2):
+                    cols = slice(g * 512 + t * P, g * 512 + (t + 1) * P)
+                    nc.tensor.matmul_mx(
+                        out=acc[:],
+                        lhsT=cd[:, cols].bitcast(FP8X4),
+                        lhsT_scale=sc[:, cols],
+                        rhs=xc[:, g * 512 : (g + 1) * 512].bitcast(FP8X4),
+                        rhs_scale=xs[:, g * 512 : (g + 1) * 512],
+                        start=(g == 0),
+                        stop=(g == 1),
+                    )
+                al.append(acc)
+            accs[j] = al
+            hps[j] = hpp.tile([P, 2048], BF16, name="hp", tag="hp")
 
         def relu(j, t, eng):
             dst = hps[j][:, t * 512 : (t + 1) * 512]
@@ -182,41 +196,38 @@ def tile_dpn_kernel(tc, x, W1, b1, W2, b2, out):
 
         acc2 = {}
 
-        def mm2(n, c, bt):
+        def mm2(n, c):
             if c == 0:
-                if bt == 0:
-                    acc2[n] = []
-                acc2[n].append(psum.tile([P, 512], F32, name="mb", tag="mb"))
-            for gg in (2 * c, 2 * c + 1):
-                if gg < 2:
-                    lc, ls, base = xc, xs, gg * 512
-                else:
-                    lc, ls, base = hc, hs, (gg - 2) * 512
-                cols = slice(base + bt * P, base + (bt + 1) * P)
-                rcols = slice(n * 5120 + gg * 512, n * 5120 + (gg + 1) * 512)
-                nc.tensor.matmul_mx(
-                    out=acc2[n][bt][:],
-                    lhsT=lc[:, cols].bitcast(FP8X4),
-                    lhsT_scale=ls[:, cols],
-                    rhs=w2c[:, rcols].bitcast(FP8X4),
-                    rhs_scale=w2s[:, rcols],
-                    start=(gg == 0),
-                    stop=(gg == 9),
-                )
+                acc2[n] = [
+                    psum.tile([P, 512], F32, name="mb", tag="mb") for bt in range(4)
+                ]
+            for bt in range(4):
+                for gg in (2 * c, 2 * c + 1):
+                    if gg < 2:
+                        lc, ls, base = xc, xs, gg * 512
+                    else:
+                        lc, ls, base = hc, hs, (gg - 2) * 512
+                    cols = slice(base + bt * P, base + (bt + 1) * P)
+                    rcols = slice(n * 5120 + gg * 512, n * 5120 + (gg + 1) * 512)
+                    nc.tensor.matmul_mx(
+                        out=acc2[n][bt][:],
+                        lhsT=lc[:, cols].bitcast(FP8X4),
+                        lhsT_scale=ls[:, cols],
+                        rhs=w2c[:, rcols].bitcast(FP8X4),
+                        rhs_scale=w2s[:, rcols],
+                        start=(gg == 0),
+                        stop=(gg == 9),
+                    )
 
-        def finish(n, bt, parts):
+        def finish(n, bt):
             ost = ostp.tile([P, 512], F32, name="ost", tag="ost")
-            step = 512 // parts
-            for lo in range(0, 512, step):
-                hi = lo + step
-                nc.vector.tensor_tensor(
-                    out=ost[:, lo:hi], in0=acc2[n][bt][:, lo:hi],
-                    in1=b2bc[:, n * 512 + lo : n * 512 + hi], op=ALU.add,
-                )
-                nc.sync.dma_start(
-                    out=out[bt * P : (bt + 1) * P, n * 512 + lo : n * 512 + hi],
-                    in_=ost[:, lo:hi],
-                )
+            nc.vector.tensor_tensor(
+                out=ost[:], in0=acc2[n][bt][:], in1=b2bc[:, n * 512 : (n + 1) * 512],
+                op=ALU.add,
+            )
+            nc.sync.dma_start(
+                out=out[bt * P : (bt + 1) * P, n * 512 : (n + 1) * 512], in_=ost[:]
+            )
 
         b1z = const.tile([P, 256], BF16, name="b1z")
         b2z = const.tile([P, OUT], BF16, name="b2z")
@@ -232,92 +243,72 @@ def tile_dpn_kernel(tc, x, W1, b1, W2, b2, out):
         make_identity(nc, ident[:])
 
         for k in range(RAW_BUFS):
-            load(k)
+            load(LOAD_ORDER[k])
 
-        g_at = (1, 2, 4, 5, 7, 8, 10, 10)
-        qh_at = (2, 3, 5, 6, 8, 9, 11, 11)
-
-        def evac_pattern(k):
-            if k < 2 or k == 18:
-                return "VSVS"
-            return "VSSS"
-
-        def t_unit(k, before_bank):
-            start_unit(k)
-            for s in range(4):
-                before_bank(s)
-                transposes(k, s)
+        def next_load(k):
             if k + RAW_BUFS < N_UNITS:
-                load(k + RAW_BUFS)
+                load(LOAD_ORDER[k + RAW_BUFS])
 
-        def nothing(s):
-            return None
-
-        def evac_quant_piece(k, s):
-            evac(k, s, evac_pattern(k)[s])
-            quant(k, s, s + 1)
-
-        t_unit(0, nothing)
-        t_unit(1, lambda s: evac_quant_piece(0, s))
+        transposes(0)
+        next_load(0)
+        evac(0, 0, "V")
+        evac(0, 1, "S")
+        evac(0, 2, "V")
+        evac(0, 3, "S")
         b1ps = psum.tile([P, 512], F32, name="mb", tag="mb")
         nc.tensor.transpose(b1ps[:, 0:P], b1z[:].bitcast(F32), ident[:])
-        b2ps = []
+        nc.vector.tensor_copy(out=b1col[:], in_=b1ps[:, 0:16].bitcast(BF16))
         for n in range(2):
-            b2ps.append(psum.tile([P, 512], F32, name="mb", tag="mb"))
+            b2ps = psum.tile([P, 512], F32, name="mb", tag="mb")
             nc.tensor.matmul(
-                out=b2ps[n][:], lhsT=ones[:], rhs=b2z[:, n * 512 : (n + 1) * 512],
+                out=b2ps[:], lhsT=ones[:], rhs=b2z[:, n * 512 : (n + 1) * 512],
                 start=True, stop=True,
             )
-        for s in range(3):
-            evac_quant_piece(1, s)
-        nc.vector.tensor_copy(out=b1col[:], in_=b1ps[:, 0:16].bitcast(BF16))
-        evac_quant_piece(1, 3)
-        for n in range(2):
-            nc.scalar.copy(out=b2bc[:, n * 512 : (n + 1) * 512], in_=b2ps[n][:])
-        mm1(0, 0)
-        mm1(0, 1)
-        relu(0, 0, "S")
-        relu(0, 1, "S")
-        t_unit(2, nothing)
-        mm1(0, 2)
-        mm1(0, 3)
-        for s in range(4):
-            evac(2, s, evac_pattern(2)[s])
-        quant(2, 0, 4)
-        relu(0, 2, "S")
-        relu(0, 3, "V")
+            nc.scalar.copy(out=b2bc[:, n * 512 : (n + 1) * 512], in_=b2ps[:])
+        quant(0)
+        transposes(1)
+        next_load(1)
+        evac(1, 0, "V")
+        evac(1, 1, "S")
+        evac(1, 2, "V")
+        evac(1, 3, "S")
+        quant(1)
 
-        for p in range(1, 18):
-            k = p + 2
-            if k < N_UNITS:
-                t_unit(k, nothing)
-            for b in range(4):
-                if p < 8:
-                    mm1(p, b)
+        pe_units = [k for k in range(N_UNITS) if k not in DV_UNITS]
+        dv_after = {
+            13: [("T", 17, 0), ("T", 17, 1)],
+            14: [("Q", 17, 0), ("Q", 17, 1)],
+        }
+
+        for p in range(18):
+            k = pe_units[p + 2] if p + 2 < len(pe_units) else None
+            if k is not None:
+                transposes(k)
+            if p + 2 < N_UNITS:
+                next_load(p + 2)
+            if p < 8:
+                mm1(p)
+            else:
+                mm2(*divmod(p - 8, 5))
+            if k is not None:
+                evac(k, 0, "V")
+                evac(k, 1, "S")
+                evac(k, 2, "S")
+                evac(k, 3, "S")
+            if 1 <= p <= 8:
+                regroup(p - 1)
+            if 2 <= p <= 9:
+                quant_h(p - 2)
+            if k is not None:
+                quant(k)
+            for what, kd, g in dv_after.get(p, []):
+                if what == "T":
+                    dv_transpose(kd, g)
                 else:
-                    n, c = divmod(p - 8, 5)
-                    mm2(n, c, b)
-            if k < N_UNITS:
-                for s in range(4):
-                    evac(k, s, evac_pattern(k)[s])
-            for j in range(8):
-                if g_at[j] == p:
-                    regroup(j)
-            for j in range(8):
-                if qh_at[j] == p:
-                    quant_h(j)
-            if p == 12:
-                finish(0, 0, 1)
-                finish(0, 1, 1)
-            if k < N_UNITS:
-                quant(k, 0, 4)
-            if p == 12:
-                finish(0, 2, 1)
-                finish(0, 3, 1)
+                    dv_quant(kd, g)
             if p < 8:
                 for t in range(4):
-                    relu(p, t, "V" if t == 3 else "S")
-            if p == 17:
-                for bt in range(3):
-                    finish(1, bt, 1)
-                finish(1, 3, 2)
+                    relu(p, t, "V" if (t == 3 and p % 2 == 1) else "S")
+            if p == 12 or p == 17:
+                for bt in range(4):
+                    finish((p - 8) // 5, bt)

@@ -109,10 +109,18 @@ def tile_dpn_kernel(tc, x, W1, b1, W2, b2, out):
                 in_=grps[k][:, g * 2048 : (g + 1) * 2048],
             )
 
-        def transposes(k):
+        def keep_warm(count):
+            for r in range(count):
+                nc.tensor.matmul(
+                    out=warm_ps[:], lhsT=ones[:], rhs=warm[:], start=True, stop=True
+                )
+
+        def transposes(k, mid=0):
             rw = raws[k][:].bitcast(F32)
             bl = []
             for s in range(4):
+                if s == 2:
+                    keep_warm(mid)
                 bank = psum.tile([P, 512], F32, name="tb", tag="tb")
                 for q in range(4):
                     nc.tensor.transpose(
@@ -235,11 +243,17 @@ def tile_dpn_kernel(tc, x, W1, b1, W2, b2, out):
         ident = const.tile([P, P], F32, name="ident")
         b1col = const.tile([P, 32], F32, name="b1col")
         b2bc = const.tile([P, OUT], F32, name="b2bc")
+        warm = const.tile([P, 512], BF16, name="warm")
+        tiny_in = const.tile([P, 8], F32, name="tiny_in")
+        tiny_out = const.tile([P, 8], F32, name="tiny_out")
+        nc.vector.memset(ones[:], 1.0)
+        nc.vector.memset(warm[:], 0.0)
         nc.vector.memset(b1z[:], 0.0)
         nc.vector.memset(b2z[:], 0.0)
-        nc.vector.memset(ones[:], 1.0)
+        nc.vector.memset(tiny_in[:], 0.0)
         nc.scalar.dma_start(out=b1z[0:16, :], in_=b1.rearrange("(a w) -> a w", a=16))
         nc.scalar.dma_start(out=b2z[0:1, :], in_=b2.rearrange("(o n) -> o n", o=1))
+        nc.scalar.activation(out=tiny_out[:], in_=tiny_in[:], func=ACT.Relu)
         make_identity(nc, ident[:])
 
         for k in range(RAW_BUFS):
@@ -249,7 +263,9 @@ def tile_dpn_kernel(tc, x, W1, b1, W2, b2, out):
             if k + RAW_BUFS < N_UNITS:
                 load(LOAD_ORDER[k + RAW_BUFS])
 
-        transposes(0)
+        warm_ps = psum.tile([P, 512], F32, name="mb", tag="mb")
+        keep_warm(5)
+        transposes(0, 1)
         next_load(0)
         evac(0, 0, "V")
         evac(0, 1, "S")
@@ -266,7 +282,8 @@ def tile_dpn_kernel(tc, x, W1, b1, W2, b2, out):
             )
             nc.scalar.copy(out=b2bc[:, n * 512 : (n + 1) * 512], in_=b2ps[:])
         quant(0)
-        transposes(1)
+        transposes(1, 1)
+        keep_warm(3)
         next_load(1)
         evac(1, 0, "V")
         evac(1, 1, "S")

from contextlib import ExitStack

import concourse.mybir as mybir
from concourse.masks import make_identity

F32 = mybir.dt.float32
BF16 = mybir.dt.bfloat16
U32 = mybir.dt.uint32
U8 = mybir.dt.uint8
FP8X4 = mybir.dt.float8_e4m3fn_x4
ACT = mybir.ActivationFunctionType
ALU = mybir.AluOpType

P = 128
B, D_IN, HID, OUT = 512, 1024, 4096, 1024
FLOPS = 2 * B * (D_IN * HID + (D_IN + HID) * OUT)

MANUAL = True
RAW_BUFS = 9
DV_UNITS = (17,)
LOAD_ORDER = tuple(range(17)) + (18, 17)
N_UNITS = 19


def tile_dpn_kernel(tc, x, W1, b1, W2, b2, out):
    nc = tc.nc
    with ExitStack() as ctx:
        const = ctx.enter_context(tc.tile_pool(name="const", bufs=1))
        keep = ctx.enter_context(tc.tile_pool(name="keep", bufs=1))
        rawp = ctx.enter_context(tc.tile_pool(name="rawp", bufs=RAW_BUFS))
        grpp = ctx.enter_context(tc.tile_pool(name="grpp", bufs=3))
        w1p = ctx.enter_context(tc.tile_pool(name="w1p", bufs=3))
        hpp = ctx.enter_context(tc.tile_pool(name="hpp", bufs=3))
        ostp = ctx.enter_context(tc.tile_pool(name="ostp", bufs=4))
        psum = ctx.enter_context(tc.psum_pool(name="psum", bufs=4))
        if MANUAL:
            ctx.enter_context(tc.manual_schedule())

        xc = keep.tile([P, 1024], U32, name="xc", align_bytes=64)
        xs = keep.tile([P, 1024], U8, name="xs", align_bytes=64)
        hc = keep.tile([P, 4096], U32, name="hc", align_bytes=64)
        hs = keep.tile([P, 4096], U8, name="hs", align_bytes=64)
        w2c = keep.tile([P, 10240], U32, name="w2c", align_bytes=64)
        w2s = keep.tile([P, 10240], U8, name="w2s", align_bytes=64)

        raws = {}
        banks = {}
        grps = {}
        codes = {0: (xc[:], xs[:])}
        for q in range(10):
            codes[9 + q] = (
                w2c[:, q * 1024 : (q + 1) * 1024],
                w2s[:, q * 1024 : (q + 1) * 1024],
            )

        def load(k):
            raw = rawp.tile([P, 4096], BF16, name="raw", tag="raw", align_bytes=64)
            raws[k] = raw
            if k in DV_UNITS:
                n, c = divmod(k - 9, 5)
                for i in range(16):
                    a, u, g = i // 4, (i // 2) % 2, i % 2
                    col = 1024 * c + 512 * g + 256 * u + 64 * a
                    nc.sync.dma_start(
                        out=raw[
                            32 * a + u : 32 * a + 32 : 2, g * 2048 : (g + 1) * 2048
                        ].rearrange("p (h w) -> p h w", w=64),
                        in_=W2[512 * n : 512 * (n + 1), col : col + 64].rearrange(
                            "(h p) w -> p h w", p=16
                        ),
                    )
            elif k == 0:
                src = x.rearrange("(s p) k -> p s k", p=P)
                dst = raw[:].rearrange("p (s k) -> p s k", s=4)
                nc.sync.dma_start(out=dst[:, 0:2, :], in_=src[:, 0:2, :])
                nc.sync.dma_start(out=dst[:, 2:4, :], in_=src[:, 2:4, :])
            elif k < 9:
                j = k - 1
                src = W1[512 * j : 512 * (j + 1), :].rearrange(
                    "(u p e) k -> p u (e k)", u=2, e=2
                )
                dst = raw[:].rearrange("p (u f) -> p u f", u=2)
                if k == 1:
                    nc.sync.dma_start(out=dst[:, 0:1, :], in_=src[:, 0:1, :])
                    nc.sync.dma_start(out=dst[:, 1:2, :], in_=src[:, 1:2, :])
                else:
                    nc.sync.dma_start(out=dst, in_=src)
            else:
                n, c = divmod(k - 9, 5)
                src = W2[
                    512 * n : 512 * (n + 1), 1024 * c : 1024 * (c + 1)
                ].rearrange("(s p) k -> p s k", p=P)
                dst = raw[:].rearrange("p (s k) -> p s k", s=4)
                nc.sync.dma_start(out=dst, in_=src)

        def dv_transpose(k, g):
            if g == 0:
                grps[k] = grpp.tile([P, 4096], BF16, name="grp", tag="grp", align_bytes=64)
            nc.vector.transpose(
                out=grps[k][:].bitcast(F32)[:, g * 1024 : (g + 1) * 1024],
                in_=raws[k][:].bitcast(F32)[:, g * 1024 : (g + 1) * 1024],
            )

        def dv_quant(k, g):
            cd, sc = codes[k]
            nc.vector.quantize_mx(
                out=cd[:, g * 512 : (g + 1) * 512].bitcast(FP8X4),
                scales=sc[:, g * 512 : (g + 1) * 512],
                in_=grps[k][:, g * 2048 : (g + 1) * 2048],
            )

        def keep_warm(count):
            for r in range(count):
                nc.tensor.matmul(
                    out=warm_ps[:], lhsT=ones[:], rhs=warm[:], start=True, stop=True
                )

        def transposes(k, mid=0):
            rw = raws[k][:].bitcast(F32)
            bl = []
            for s in range(4):
                if s == 2:
                    keep_warm(mid)
                bank = psum.tile([P, 512], F32, name="tb", tag="tb")
                for q in range(4):
                    nc.tensor.transpose(
                        bank[:, q * P : (q + 1) * P],
                        rw[:, s * 512 + q * P : s * 512 + (q + 1) * P],
                        ident[:],
                    )
                bl.append(bank)
            banks[k] = bl
            grps[k] = grpp.tile([P, 4096], BF16, name="grp", tag="grp", align_bytes=64)

        def evac(k, s, eng):
            dst = grps[k][:].bitcast(F32).rearrange(
                "p (g s r u) -> p g s r u", g=2, s=4, u=2
            )[:, :, s]
            src = banks[k][s][:].rearrange("p (g u r) -> p g r u", g=2, u=2)
            if eng == "V":
                nc.vector.tensor_copy(out=dst, in_=src)
            else:
                nc.scalar.copy(out=dst, in_=src)

        def quant(k):
            if 1 <= k < 9:
                w1c = w1p.tile([P, 1024], U32, name="w1c", tag="w1c", align_bytes=64)
                w1s = w1p.tile([P, 1024], U8, name="w1s", tag="w1s", align_bytes=64)
                codes[k] = (w1c[:], w1s[:])
            cd, sc = codes[k]
            nc.vector.quantize_mx(out=cd.bitcast(FP8X4), scales=sc, in_=grps[k][:])

        accs = {}
        hps = {}
        hgs = {}

        def mm1(j):
            cd, sc = codes[1 + j]
            al = []
            for t in range(4):
                acc = psum.tile([P, 512], F32, name="mb", tag="mb")
                for g in range(2):
                    cols = slice(g * 512 + t * P, g * 512 + (t + 1) * P)
                    nc.tensor.matmul_mx(
                        out=acc[:],
                        lhsT=cd[:, cols].bitcast(FP8X4),
                        lhsT_scale=sc[:, cols],
                        rhs=xc[:, g * 512 : (g + 1) * 512].bitcast(FP8X4),
                        rhs_scale=xs[:, g * 512 : (g + 1) * 512],
                        start=(g == 0),
                        stop=(g == 1),
                    )
                al.append(acc)
            accs[j] = al
            hps[j] = hpp.tile([P, 2048], BF16, name="hp", tag="hp")

        def relu(j, t, eng):
            dst = hps[j][:, t * 512 : (t + 1) * 512]
            bias = b1col[:, 4 * j + t : 4 * j + t + 1]
            if eng == "V":
                nc.vector.tensor_scalar(
                    out=dst, in0=accs[j][t][:], scalar1=bias, scalar2=0.0,
                    op0=ALU.add, op1=ALU.max,
                )
            else:
                nc.scalar.activation(
                    out=dst, in_=accs[j][t][:], func=ACT.Relu, bias=bias, scale=1.0
                )

        def regroup(j):
            hg = hpp.tile([P, 2048], BF16, name="hg", tag="hg", align_bytes=64)
            hgs[j] = hg
            nc.vector.tensor_copy(
                out=hg[:].rearrange("p (c i t) -> p c t i", i=4, t=4),
                in_=hps[j][:].rearrange("p (t c i) -> p c t i", t=4, i=4),
            )

        def quant_h(j):
            nc.vector.quantize_mx(
                out=hc[:, j * 512 : (j + 1) * 512].bitcast(FP8X4),
                scales=hs[:, j * 512 : (j + 1) * 512],
                in_=hgs[j][:],
            )

        acc2 = {}

        def mm2(n, c):
            if c == 0:
                acc2[n] = [
                    psum.tile([P, 512], F32, name="mb", tag="mb") for bt in range(4)
                ]
            for bt in range(4):
                for gg in (2 * c, 2 * c + 1):
                    if gg < 2:
                        lc, ls, base = xc, xs, gg * 512
                    else:
                        lc, ls, base = hc, hs, (gg - 2) * 512
                    cols = slice(base + bt * P, base + (bt + 1) * P)
                    rcols = slice(n * 5120 + gg * 512, n * 5120 + (gg + 1) * 512)
                    nc.tensor.matmul_mx(
                        out=acc2[n][bt][:],
                        lhsT=lc[:, cols].bitcast(FP8X4),
                        lhsT_scale=ls[:, cols],
                        rhs=w2c[:, rcols].bitcast(FP8X4),
                        rhs_scale=w2s[:, rcols],
                        start=(gg == 0),
                        stop=(gg == 9),
                    )

        def finish(n, bt):
            ost = ostp.tile([P, 512], F32, name="ost", tag="ost")
            nc.vector.tensor_tensor(
                out=ost[:], in0=acc2[n][bt][:], in1=b2bc[:, n * 512 : (n + 1) * 512],
                op=ALU.add,
            )
            nc.sync.dma_start(
                out=out[bt * P : (bt + 1) * P, n * 512 : (n + 1) * 512], in_=ost[:]
            )

        b1z = const.tile([P, 256], BF16, name="b1z")
        b2z = const.tile([P, OUT], BF16, name="b2z")
        ones = const.tile([P, P], BF16, name="ones")
        ident = const.tile([P, P], F32, name="ident")
        b1col = const.tile([P, 32], F32, name="b1col")
        b2bc = const.tile([P, OUT], F32, name="b2bc")
        warm = const.tile([P, 512], BF16, name="warm")
        tiny_in = const.tile([P, 8], F32, name="tiny_in")
        tiny_out = const.tile([P, 8], F32, name="tiny_out")
        nc.vector.memset(ones[:], 1.0)
        nc.vector.memset(warm[:], 0.0)
        nc.vector.memset(b1z[:], 0.0)
        nc.vector.memset(b2z[:], 0.0)
        nc.vector.memset(tiny_in[:], 0.0)
        nc.scalar.dma_start(out=b1z[0:16, :], in_=b1.rearrange("(a w) -> a w", a=16))
        nc.scalar.dma_start(out=b2z[0:1, :], in_=b2.rearrange("(o n) -> o n", o=1))
        nc.scalar.activation(out=tiny_out[:], in_=tiny_in[:], func=ACT.Relu)
        make_identity(nc, ident[:])

        for k in range(RAW_BUFS):
            load(LOAD_ORDER[k])

        def next_load(k):
            if k + RAW_BUFS < N_UNITS:
                load(LOAD_ORDER[k + RAW_BUFS])

        warm_ps = psum.tile([P, 512], F32, name="mb", tag="mb")
        keep_warm(5)
        transposes(0, 1)
        next_load(0)
        evac(0, 0, "V")
        evac(0, 1, "S")
        evac(0, 2, "V")
        evac(0, 3, "S")
        b1ps = psum.tile([P, 512], F32, name="mb", tag="mb")
        nc.tensor.transpose(b1ps[:, 0:P], b1z[:].bitcast(F32), ident[:])
        nc.vector.tensor_copy(out=b1col[:], in_=b1ps[:, 0:16].bitcast(BF16))
        for n in range(2):
            b2ps = psum.tile([P, 512], F32, name="mb", tag="mb")
            nc.tensor.matmul(
                out=b2ps[:], lhsT=ones[:], rhs=b2z[:, n * 512 : (n + 1) * 512],
                start=True, stop=True,
            )
            nc.scalar.copy(out=b2bc[:, n * 512 : (n + 1) * 512], in_=b2ps[:])
        quant(0)
        transposes(1, 1)
        keep_warm(3)
        next_load(1)
        evac(1, 0, "V")
        evac(1, 1, "S")
        evac(1, 2, "V")
        evac(1, 3, "S")
        quant(1)

        pe_units = [k for k in range(N_UNITS) if k not in DV_UNITS]
        dv_after = {
            13: [("T", 17, 0), ("T", 17, 1)],
            14: [("Q", 17, 0), ("Q", 17, 1)],
        }

        for p in range(18):
            k = pe_units[p + 2] if p + 2 < len(pe_units) else None
            if k is not None:
                transposes(k)
            if p + 2 < N_UNITS:
                next_load(p + 2)
            if p < 8:
                mm1(p)
            else:
                mm2(*divmod(p - 8, 5))
            if k is not None:
                evac(k, 0, "V")
                evac(k, 1, "S")
                evac(k, 2, "S")
                evac(k, 3, "S")
            if 1 <= p <= 8:
                regroup(p - 1)
            if 2 <= p <= 9:
                quant_h(p - 2)
            if k is not None:
                quant(k)
            for what, kd, g in dv_after.get(p, []):
                if what == "T":
                    dv_transpose(kd, g)
                else:
                    dv_quant(kd, g)
            if p < 8:
                for t in range(4):
                    relu(p, t, "V" if (t == 3 and p % 2 == 1) else "S")
            if p == 12 or p == 17:
                for bt in range(4):
                    finish((p - 8) // 5, bt)
